import numpy as np
import ml_dtypes


def mxq(x, axis, fmt="e4m3"):
    dtype, down = {"e4m3": (ml_dtypes.float8_e4m3fn, 7), "e5m2": (ml_dtypes.float8_e5m2, 14)}[fmt]
    v = np.moveaxis(np.asarray(x, np.float32).astype(ml_dtypes.bfloat16).astype(np.float64), axis, -1)
    blocks = v.reshape(v.shape[:-1] + (-1, 32))
    amax = np.abs(blocks).max(-1, keepdims=True)
    byte = np.maximum(np.where(amax > 0, np.frexp(amax)[1] - 1 + 127, 0) - down, 1)
    scale = np.exp2(byte - 127.0)
    codes = (blocks / scale).astype(np.float32).astype(dtype).astype(np.float64)
    return np.moveaxis((codes * scale).reshape(v.shape), -1, axis)


WIDE = False


def mx_kscale(k):
    if not WIDE:
        return np.ones(k)
    levels = np.array([10, -10, 5, -5, 0])
    a = np.random.permutation(np.resize(levels, k // 512 * 4)).reshape(k // 512, 4)
    idx = np.arange(k)
    return np.exp2(a[idx // 512, idx % 128 // 32])


BF16 = ml_dtypes.bfloat16


def bf(x):
    return np.asarray(x, np.float32).astype(BF16)


def f64(x):
    return np.asarray(x).astype(np.float64)


T, S, B, E, Z = 2048, 512, 4, 512, 128


def sigmoid(v):
    return 1.0 / (1.0 + np.exp(-v))


def setup_inputs():
    t = mx_kscale(E)
    return {"query": bf(np.random.standard_normal((T, B, E))),
            "hr": bf(np.random.standard_normal((T, B, E)) * 0.2 * t),
            "Wu": bf(np.random.standard_normal((E, E)) / np.sqrt(E)),
            "bu": bf(np.random.standard_normal(E) * 0.3),
            "Wh": bf(np.random.standard_normal((E, E)) * 5.0 / np.sqrt(E) / t[None, :]),
            "bh": bf(np.random.standard_normal(E) * 0.3)}


def reference(query, hr, Wu, bu, Wh, bh):
    x = f64(query)
    u = sigmoid((mxq(x, 2, "e4m3") @ mxq(f64(Wu), 1, "e4m3").T) + f64(bu))
    h = np.tanh((mxq(f64(hr), 2, "e4m3") @ mxq(f64(Wh), 1, "e4m3").T) + f64(bh))
    return x + u * (h - x)

@@ -1,0 +1,204 @@
+from contextlib import ExitStack
+
+import concourse.bass as bass
+import concourse.mybir as mybir
+import concourse.tile as tile
+from concourse.masks import make_identity
+
+F32 = mybir.dt.float32
+BF16 = mybir.dt.bfloat16
+U32 = mybir.dt.uint32
+U8 = mybir.dt.uint8
+FP8X4 = mybir.dt.float8_e4m3fn_x4
+ACT = mybir.ActivationFunctionType
+ALU = mybir.AluOpType
+
+P = 128
+E = 512
+ROWS = 8192
+RG = 512
+NG = ROWS // RG
+NT = 4
+FLOPS = 2 * 2 * ROWS * E * E
+
+G_COLS = 0
+
+
+def tile_gatedcrossattention_pb_t_kernel(tc, query, hr, Wu, bu, Wh, bh, out):
+    nc = tc.nc
+    xf = query.rearrange("t b e -> (t b) e")
+    hf = hr.rearrange("t b e -> (t b) e")
+    of = out.rearrange("t b e -> (t b) e")
+
+    with ExitStack() as ctx:
+        const = ctx.enter_context(tc.tile_pool(name="const", bufs=1))
+        rows = ctx.enter_context(tc.tile_pool(name="rows", bufs=3))
+        work = ctx.enter_context(tc.tile_pool(name="work", bufs=3))
+        psum = ctx.enter_context(tc.psum_pool(name="psum", bufs=2))
+        ctx.enter_context(tc.manual_schedule())
+
+        zero1 = const.tile([P, 1], F32, name="zero1")
+        nc.vector.memset(zero1[:], 0.0)
+        warm = const.tile([P, 1], F32, name="warm")
+        nc.scalar.activation(out=warm[:], in_=zero1[:], func=ACT.Sigmoid)
+        ident = const.tile([P, P], F32, name="ident")
+        make_identity(nc, ident[:])
+        brow = const.tile([P, 2 * P], BF16, name="brow")
+        nc.vector.memset(brow[:], 0.0)
+        nc.scalar.dma_start(out=brow[0:2, :], in_=bu.rearrange("(u c) -> u c", u=2))
+        nc.scalar.dma_start(out=brow[2:4, :], in_=bh.rearrange("(u c) -> u c", u=2))
+
+        x_sb = {}
+        h_sb = {}
+        gx = {}
+        codes = {}
+        planes = {}
+        gate = {}
+        cand = {}
+
+        def load(g):
+            if g < 0 or g >= NG:
+                return
+            ht = rows.tile([P, NT * E], BF16, name="hrow%d" % g, tag="hrow", bufs=3)
+            nc.sync.dma_start(out=ht[:], in_=hf[g * RG:(g + 1) * RG, :].rearrange("(p j) e -> p (j e)", j=NT))
+            h_sb[g] = ht
+            xt = rows.tile([P, NT * E], BF16, name="xrow%d" % g, tag="xrow", bufs=6)
+            nc.sync.dma_start(out=xt[:], in_=xf[g * RG:(g + 1) * RG, :].rearrange("(p j) e -> p (j e)", j=NT))
+            x_sb[g] = xt
+
+        def forward(src, key, tag, bufs, engines):
+            grouped = work.tile([P, NT * E], BF16, name="grp_%s" % key, tag="grp_" + tag, bufs=bufs, align_bytes=64)
+            sw = src[:].bitcast(F32)
+            gw = grouped[:].bitcast(F32)
+            for b in range(2):
+                bank = psum.tile([P, 512], F32, name="tp_%s_%d" % (key, b), tag="tp", bufs=2)
+                for u in range(2):
+                    for jj in range(2):
+                        j = 2 * b + jj
+                        nc.tensor.transpose(
+                            bank[:, u * 256 + jj * P:u * 256 + (jj + 1) * P],
+                            sw[:, j * 256 + u * P:j * 256 + (u + 1) * P],
+                            ident[:],
+                        )
+                dst = gw[:, b * 512:(b + 1) * 512].rearrange("p (r u) -> p r u", u=2)
+                srcv = bank[:].rearrange("p (u r) -> p r u", u=2)
+                if engines[b] == "S":
+                    nc.scalar.copy(out=dst, in_=srcv)
+                else:
+                    nc.vector.tensor_copy(out=dst, in_=srcv)
+            return grouped
+
+        def quantise(grouped, key, tag, bufs):
+            cw = work.tile([P, 512], U32, name="cw_%s" % key, tag="cw_" + tag, bufs=bufs, align_bytes=64)
+            sp = work.tile([P, 512], U8, name="sp_%s" % key, tag="sp_" + tag, bufs=bufs, align_bytes=64)
+            nc.vector.quantize_mx(out=cw[:].bitcast(FP8X4), scales=sp[:], in_=grouped[:])
+            codes[key] = cw
+            planes[key] = sp
+
+        w_sb = {}
+        for name, w in (("wh", Wh), ("wu", Wu)):
+            wt = const.tile([P, NT * E], BF16, name="row_" + name)
+            nc.sync.dma_start(
+                out=wt[:].rearrange("m (u e k) -> m u e k", u=2, e=2),
+                in_=w.rearrange("(u m e) k -> m u e k", u=2, e=2),
+            )
+            w_sb[name] = wt
+        load(0)
+        bank = psum.tile([P, 512], F32, name="tp_bias", tag="tp", bufs=2)
+        nc.tensor.transpose(bank[:, 0:P], brow[:].bitcast(F32), ident[:])
+        bias = const.tile([P, 8], F32, name="bias")
+        nc.vector.tensor_copy(out=bias[:], in_=bank[:, 0:4].bitcast(BF16))
+        for name in ("wh", "wu"):
+            gw_ = forward(w_sb[name], name, name, 1, ("S", "V"))
+            quantise(gw_, name, name, 1)
+
+        grp_h = {}
+
+        def fwd_h(g, engines):
+            if 0 <= g < NG:
+                grp_h[g] = forward(h_sb[g], "h%d" % g, "h", 2, engines)
+
+        def fwd_x(g, engines):
+            if 0 <= g < NG:
+                gx[g] = forward(x_sb[g], "x%d" % g, "x", 4, engines)
+
+        def quant(g):
+            if 0 <= g < NG:
+                quantise(grp_h[g], "h%d" % g, "h", 3)
+                quantise(gx[g], "x%d" % g, "x", 3)
+
+        def mx(g, wname, key, dst, func, bcol):
+            for t in range(NT):
+                z = psum.tile([P, 512], F32, name="z_%s_%d" % (key, t), tag="z", bufs=4)
+                nc.tensor.matmul_mx(
+                    out=z[:],
+                    lhsT=codes[wname][:, t * P:(t + 1) * P].bitcast(FP8X4),
+                    lhsT_scale=planes[wname][:, t * P:(t + 1) * P],
+                    rhs=codes[key][:].bitcast(FP8X4),
+                    rhs_scale=planes[key][:],
+                    start=True,
+                    stop=True,
+                )
+                nc.scalar.activation(
+                    out=dst[:, t * RG:(t + 1) * RG], in_=z[:], func=func,
+                    bias=bias[:, bcol + t:bcol + t + 1], scale=1.0,
+                )
+
+        o_sb = {}
+
+        def back(g, js):
+            if g < 0 or g >= NG:
+                return
+            if g not in o_sb:
+                o_sb[g] = rows.tile([P, NT * E], F32, name="orow%d" % g, tag="orow", bufs=3)
+            for j in js:
+                ot = psum.tile([P, 512], F32, name="ot_%d_%d" % (g, j), tag="ot", bufs=2)
+                for t in range(NT):
+                    nc.tensor.transpose(
+                        ot[:, t * P:(t + 1) * P],
+                        cand[g][:, t * RG + j * P:t * RG + (j + 1) * P],
+                        ident[:],
+                    )
+                nc.vector.tensor_tensor(
+                    out=o_sb[g][:, j * E:(j + 1) * E].rearrange("p (u m e) -> p u m e", u=2, e=2),
+                    in0=ot[:].rearrange("p (u e m) -> p u m e", u=2, e=2),
+                    in1=x_sb[g][:, j * E:(j + 1) * E].rearrange("p (u m e) -> p u m e", u=2, e=2),
+                    op=ALU.add,
+                )
+
+        def store(g):
+            if 0 <= g < NG:
+                nc.sync.dma_start(
+                    out=of[g * RG:(g + 1) * RG, :].rearrange("(p j) e -> p (j e)", j=NT), in_=o_sb[g][:]
+                )
+
+        for i in range(-2, NG + 1):
+            early = i < 0
+            eng = ("S", "V") if early else ("S", "S")
+            load(i + 3)
+            live = 0 <= i < NG
+            if live:
+                cand[i] = work.tile([P, NT * RG], F32, name="cand%d" % i, tag="cand", bufs=3)
+                mx(i, "wh", "h%d" % i, cand[i], ACT.Tanh, 4)
+            fwd_h(i + 2, eng)
+            if live:
+                gate[i] = work.tile([P, NT * RG], F32, name="gate%d" % i, tag="gate", bufs=2)
+                mx(i, "wu", "x%d" % i, gate[i], ACT.Sigmoid, 0)
+                c3 = cand[i][:].rearrange("p (t r) -> p t r", t=NT)
+                nc.vector.tensor_tensor(
+                    out=c3, in0=c3, in1=gx[i][:].rearrange("p (r t) -> p t r", t=NT), op=ALU.subtract
+                )
+            back(i - 1, (0, 1))
+            fwd_x(i + 2, eng)
+            back(i - 1, (2, 3))
+            store(i - 1)
+            if live:
+                split = NT * RG - G_COLS
+                nc.vector.tensor_tensor(
+                    out=cand[i][:, 0:split], in0=gate[i][:, 0:split], in1=cand[i][:, 0:split], op=ALU.mult
+                )
+                if G_COLS:
+                    nc.gpsimd.tensor_tensor(
+                        out=cand[i][:, split:], in0=gate[i][:, split:], in1=cand[i][:, split:], op=ALU.mult
+                    )
+            quant(i + 2)

@@ -21,7 +21,11 @@ NG = ROWS // RG
 NT = 4
 FLOPS = 2 * 2 * ROWS * E * E
 
-G_COLS = 0
+G_COLS = 1024
+LAG = 2
+Z_BUFS = 3
+OT_BUFS = 3
+TP_BUFS = 2
 
 
 def tile_gatedcrossattention_pb_t_kernel(tc, query, hr, Wu, bu, Wh, bh, out):
@@ -37,41 +41,50 @@ def tile_gatedcrossattention_pb_t_kernel(tc, query, hr, Wu, bu, Wh, bh, out):
         psum = ctx.enter_context(tc.psum_pool(name="psum", bufs=2))
         ctx.enter_context(tc.manual_schedule())
 
+        brow = const.tile([P, 2 * P], BF16, name="brow")
+        nc.vector.memset(brow[:], 0.0)
         zero1 = const.tile([P, 1], F32, name="zero1")
         nc.vector.memset(zero1[:], 0.0)
+        nc.sync.dma_start(out=brow[0:2, :], in_=bu.rearrange("(u c) -> u c", u=2))
+        nc.sync.dma_start(out=brow[2:4, :], in_=bh.rearrange("(u c) -> u c", u=2))
         warm = const.tile([P, 1], F32, name="warm")
         nc.scalar.activation(out=warm[:], in_=zero1[:], func=ACT.Sigmoid)
         ident = const.tile([P, P], F32, name="ident")
         make_identity(nc, ident[:])
-        brow = const.tile([P, 2 * P], BF16, name="brow")
-        nc.vector.memset(brow[:], 0.0)
-        nc.scalar.dma_start(out=brow[0:2, :], in_=bu.rearrange("(u c) -> u c", u=2))
-        nc.scalar.dma_start(out=brow[2:4, :], in_=bh.rearrange("(u c) -> u c", u=2))
 
-        x_sb = {}
-        h_sb = {}
-        gx = {}
+        src_sb = {}
+        grp = {}
         codes = {}
         planes = {}
         gate = {}
         cand = {}
+        o_sb = {}
 
-        def load(g):
+        def load_w(name, w):
+            wt = const.tile([P, NT * E], BF16, name="row_" + name)
+            nc.sync.dma_start(
+                out=wt[:].rearrange("m (u e k) -> m u e k", u=2, e=2),
+                in_=w.rearrange("(u m e) k -> m u e k", u=2, e=2),
+            )
+            src_sb[name] = wt
+
+        def load_rows(kind, g):
             if g < 0 or g >= NG:
                 return
-            ht = rows.tile([P, NT * E], BF16, name="hrow%d" % g, tag="hrow", bufs=3)
-            nc.sync.dma_start(out=ht[:], in_=hf[g * RG:(g + 1) * RG, :].rearrange("(p j) e -> p (j e)", j=NT))
-            h_sb[g] = ht
-            xt = rows.tile([P, NT * E], BF16, name="xrow%d" % g, tag="xrow", bufs=6)
-            nc.sync.dma_start(out=xt[:], in_=xf[g * RG:(g + 1) * RG, :].rearrange("(p j) e -> p (j e)", j=NT))
-            x_sb[g] = xt
+            srcf = hf if kind == "h" else xf
+            rt = rows.tile([P, NT * E], BF16, name="%srow%d" % (kind, g), tag=kind + "row", bufs=(3 if kind == "h" else 6))
+            nc.sync.dma_start(out=rt[:], in_=srcf[g * RG:(g + 1) * RG, :].rearrange("(p j) e -> p (j e)", j=NT))
+            src_sb["%s%d" % (kind, g)] = rt
 
-        def forward(src, key, tag, bufs, engines):
-            grouped = work.tile([P, NT * E], BF16, name="grp_%s" % key, tag="grp_" + tag, bufs=bufs, align_bytes=64)
-            sw = src[:].bitcast(F32)
+        GRP_BUFS = {"wh": 1, "wu": 1, "h": 2, "x": LAG + 2}
+        Q_BUFS = {"wh": 1, "wu": 1, "h": LAG + 1, "x": LAG + 1}
+
+        def forward(key, tag, engines):
+            grouped = work.tile([P, NT * E], BF16, name="grp_%s" % key, tag="grp_" + tag, bufs=GRP_BUFS[tag], align_bytes=64)
+            sw = src_sb[key][:].bitcast(F32)
             gw = grouped[:].bitcast(F32)
             for b in range(2):
-                bank = psum.tile([P, 512], F32, name="tp_%s_%d" % (key, b), tag="tp", bufs=2)
+                bank = psum.tile([P, 512], F32, name="tp_%s_%d" % (key, b), tag="tp", bufs=TP_BUFS)
                 for u in range(2):
                     for jj in range(2):
                         j = 2 * b + jj
@@ -86,50 +99,33 @@ def tile_gatedcrossattention_pb_t_kernel(tc, query, hr, Wu, bu, Wh, bh, out):
                     nc.scalar.copy(out=dst, in_=srcv)
                 else:
                     nc.vector.tensor_copy(out=dst, in_=srcv)
-            return grouped
+            grp[key] = grouped
 
-        def quantise(grouped, key, tag, bufs):
-            cw = work.tile([P, 512], U32, name="cw_%s" % key, tag="cw_" + tag, bufs=bufs, align_bytes=64)
-            sp = work.tile([P, 512], U8, name="sp_%s" % key, tag="sp_" + tag, bufs=bufs, align_bytes=64)
-            nc.vector.quantize_mx(out=cw[:].bitcast(FP8X4), scales=sp[:], in_=grouped[:])
+        def quantise(key, tag):
+            cw = work.tile([P, 512], U32, name="cw_%s" % key, tag="cw_" + tag, bufs=Q_BUFS[tag], align_bytes=64)
+            sp = work.tile([P, 512], U8, name="sp_%s" % key, tag="sp_" + tag, bufs=Q_BUFS[tag], align_bytes=64)
+            nc.vector.quantize_mx(out=cw[:].bitcast(FP8X4), scales=sp[:], in_=grp[key][:])
             codes[key] = cw
             planes[key] = sp
 
-        w_sb = {}
-        for name, w in (("wh", Wh), ("wu", Wu)):
-            wt = const.tile([P, NT * E], BF16, name="row_" + name)
-            nc.sync.dma_start(
-                out=wt[:].rearrange("m (u e k) -> m u e k", u=2, e=2),
-                in_=w.rearrange("(u m e) k -> m u e k", u=2, e=2),
-            )
-            w_sb[name] = wt
-        load(0)
-        bank = psum.tile([P, 512], F32, name="tp_bias", tag="tp", bufs=2)
-        nc.tensor.transpose(bank[:, 0:P], brow[:].bitcast(F32), ident[:])
+        def fwd(kind, g, engines):
+            if 0 <= g < NG:
+                forward("%s%d" % (kind, g), kind, engines)
+
+        def quant(kind, g):
+            if 0 <= g < NG:
+                quantise("%s%d" % (kind, g), kind)
+
         bias = const.tile([P, 8], F32, name="bias")
-        nc.vector.tensor_copy(out=bias[:], in_=bank[:, 0:4].bitcast(BF16))
-        for name in ("wh", "wu"):
-            gw_ = forward(w_sb[name], name, name, 1, ("S", "V"))
-            quantise(gw_, name, name, 1)
 
-        grp_h = {}
+        def make_bias():
+            bank = psum.tile([P, 512], F32, name="tp_bias", tag="tp", bufs=TP_BUFS)
+            nc.tensor.transpose(bank[:, 0:P], brow[:].bitcast(F32), ident[:])
+            nc.vector.tensor_copy(out=bias[:], in_=bank[:, 0:4].bitcast(BF16))
 
-        def fwd_h(g, engines):
-            if 0 <= g < NG:
-                grp_h[g] = forward(h_sb[g], "h%d" % g, "h", 2, engines)
-
-        def fwd_x(g, engines):
-            if 0 <= g < NG:
-                gx[g] = forward(x_sb[g], "x%d" % g, "x", 4, engines)
-
-        def quant(g):
-            if 0 <= g < NG:
-                quantise(grp_h[g], "h%d" % g, "h", 3)
-                quantise(gx[g], "x%d" % g, "x", 3)
-
-        def mx(g, wname, key, dst, func, bcol):
+        def mx(wname, key, dst, func, bcol):
             for t in range(NT):
-                z = psum.tile([P, 512], F32, name="z_%s_%d" % (key, t), tag="z", bufs=4)
+                z = psum.tile([P, 512], F32, name="z_%s_%d" % (key, t), tag="z", bufs=Z_BUFS)
                 nc.tensor.matmul_mx(
                     out=z[:],
                     lhsT=codes[wname][:, t * P:(t + 1) * P].bitcast(FP8X4),
@@ -144,15 +140,13 @@ def tile_gatedcrossattention_pb_t_kernel(tc, query, hr, Wu, bu, Wh, bh, out):
                     bias=bias[:, bcol + t:bcol + t + 1], scale=1.0,
                 )
 
-        o_sb = {}
-
         def back(g, js):
             if g < 0 or g >= NG:
                 return
             if g not in o_sb:
                 o_sb[g] = rows.tile([P, NT * E], F32, name="orow%d" % g, tag="orow", bufs=3)
             for j in js:
-                ot = psum.tile([P, 512], F32, name="ot_%d_%d" % (g, j), tag="ot", bufs=2)
+                ot = psum.tile([P, 512], F32, name="ot_%d_%d" % (g, j), tag="ot", bufs=OT_BUFS)
                 for t in range(NT):
                     nc.tensor.transpose(
                         ot[:, t * P:(t + 1) * P],
@@ -162,9 +156,14 @@ def tile_gatedcrossattention_pb_t_kernel(tc, query, hr, Wu, bu, Wh, bh, out):
                 nc.vector.tensor_tensor(
                     out=o_sb[g][:, j * E:(j + 1) * E].rearrange("p (u m e) -> p u m e", u=2, e=2),
                     in0=ot[:].rearrange("p (u e m) -> p u m e", u=2, e=2),
-                    in1=x_sb[g][:, j * E:(j + 1) * E].rearrange("p (u m e) -> p u m e", u=2, e=2),
+                    in1=src_sb["x%d" % g][:, j * E:(j + 1) * E].rearrange("p (u m e) -> p u m e", u=2, e=2),
                     op=ALU.add,
                 )
+                if g == NG - 1:
+                    nc.sync.dma_start(
+                        out=of[g * RG:(g + 1) * RG, :].rearrange("(p j) e -> p j e", j=NT)[:, j, :],
+                        in_=o_sb[g][:, j * E:(j + 1) * E],
+                    )
 
         def store(g):
             if 0 <= g < NG:
@@ -172,33 +171,55 @@ def tile_gatedcrossattention_pb_t_kernel(tc, query, hr, Wu, bu, Wh, bh, out):
                     out=of[g * RG:(g + 1) * RG, :].rearrange("(p j) e -> p (j e)", j=NT), in_=o_sb[g][:]
                 )
 
-        for i in range(-2, NG + 1):
-            early = i < 0
-            eng = ("S", "V") if early else ("S", "S")
-            load(i + 3)
+        load_w("wh", Wh)
+        load_rows("h", 0)
+        load_w("wu", Wu)
+        load_rows("x", 0)
+        for g in range(1, 3):
+            load_rows("h", g)
+            load_rows("x", g)
+        SV = ("S", "V")
+        forward("wh", "wh", SV)
+        fwd("h", 0, SV)
+        quantise("wh", "wh")
+        quant("h", 0)
+        make_bias()
+        forward("wu", "wu", SV)
+        fwd("x", 0, SV)
+        quantise("wu", "wu")
+        quant("x", 0)
+        for g in range(1, LAG):
+            fwd("h", g, SV)
+            fwd("x", g, SV)
+            quant("h", g)
+            quant("x", g)
+        for i in range(0, NG + 1):
+            eng = ("S", "S")
+            load_rows("h", i + 3)
+            load_rows("x", i + 3)
             live = 0 <= i < NG
             if live:
                 cand[i] = work.tile([P, NT * RG], F32, name="cand%d" % i, tag="cand", bufs=3)
-                mx(i, "wh", "h%d" % i, cand[i], ACT.Tanh, 4)
-            fwd_h(i + 2, eng)
-            if live:
+                mx("wh", "h%d" % i, cand[i], ACT.Tanh, 4)
                 gate[i] = work.tile([P, NT * RG], F32, name="gate%d" % i, tag="gate", bufs=2)
-                mx(i, "wu", "x%d" % i, gate[i], ACT.Sigmoid, 0)
+                mx("wu", "x%d" % i, gate[i], ACT.Sigmoid, 0)
                 c3 = cand[i][:].rearrange("p (t r) -> p t r", t=NT)
                 nc.vector.tensor_tensor(
-                    out=c3, in0=c3, in1=gx[i][:].rearrange("p (r t) -> p t r", t=NT), op=ALU.subtract
+                    out=c3, in0=c3, in1=grp["x%d" % i][:].rearrange("p (r t) -> p t r", t=NT), op=ALU.subtract
                 )
-            back(i - 1, (0, 1))
-            fwd_x(i + 2, eng)
-            back(i - 1, (2, 3))
-            store(i - 1)
-            if live:
-                split = NT * RG - G_COLS
-                nc.vector.tensor_tensor(
-                    out=cand[i][:, 0:split], in0=gate[i][:, 0:split], in1=cand[i][:, 0:split], op=ALU.mult
-                )
-                if G_COLS:
+                split = NT * RG - (G_COLS if i > 0 else 0)
+                if split < NT * RG:
                     nc.gpsimd.tensor_tensor(
                         out=cand[i][:, split:], in0=gate[i][:, split:], in1=cand[i][:, split:], op=ALU.mult
                     )
-            quant(i + 2)
+            fwd("h", i + LAG, eng)
+            back(i - 1, (0, 1, 2))
+            fwd("x", i + LAG, eng)
+            back(i - 1, (3,))
+            if live:
+                store(i - 1)
+                nc.vector.tensor_tensor(
+                    out=cand[i][:, 0:split], in0=gate[i][:, 0:split], in1=cand[i][:, 0:split], op=ALU.mult
+                )
+            quant("h", i + LAG)
+            quant("x", i + LAG)

@@ -21,10 +21,10 @@ NG = ROWS // RG
 NT = 4
 FLOPS = 2 * 2 * ROWS * E * E
 
-G_COLS = 1024
-LAG = 2
+G_COLS = 0
+LAG = 3
 Z_BUFS = 3
-OT_BUFS = 3
+OT_BUFS = 2
 TP_BUFS = 2
 
 
@@ -72,19 +72,24 @@ def tile_gatedcrossattention_pb_t_kernel(tc, query, hr, Wu, bu, Wh, bh, out):
             if g < 0 or g >= NG:
                 return
             srcf = hf if kind == "h" else xf
-            rt = rows.tile([P, NT * E], BF16, name="%srow%d" % (kind, g), tag=kind + "row", bufs=(3 if kind == "h" else 6))
+            rt = rows.tile([P, NT * E], BF16, name="%srow%d" % (kind, g), tag=kind + "row", bufs=(4 if kind == "h" else 7))
             nc.sync.dma_start(out=rt[:], in_=srcf[g * RG:(g + 1) * RG, :].rearrange("(p j) e -> p (j e)", j=NT))
             src_sb["%s%d" % (kind, g)] = rt
 
-        GRP_BUFS = {"wh": 1, "wu": 1, "h": 2, "x": LAG + 2}
+        GRP_BUFS = {"wh": 1, "wu": 1, "h": 2, "x": 2}
         Q_BUFS = {"wh": 1, "wu": 1, "h": LAG + 1, "x": LAG + 1}
 
-        def forward(key, tag, engines):
-            grouped = work.tile([P, NT * E], BF16, name="grp_%s" % key, tag="grp_" + tag, bufs=GRP_BUFS[tag], align_bytes=64)
+        banks = {}
+
+        PS_TAG = {"w": "xt", "x": "xt", "h": "ht"}
+        PS_BUFS = {"w": 2, "x": 2, "h": 1}
+
+        ALL_BUFS = {"xt": 2, "ht": 1, "z": Z_BUFS, "ot": OT_BUFS}
+
+        def turn(key, bs=(0, 1), tag=None):
             sw = src_sb[key][:].bitcast(F32)
-            gw = grouped[:].bitcast(F32)
-            for b in range(2):
-                bank = psum.tile([P, 512], F32, name="tp_%s_%d" % (key, b), tag="tp", bufs=TP_BUFS)
+            for b in bs:
+                bank = psum.tile([P, 512], F32, name="tp_%s_%d" % (key, b), tag=(tag or PS_TAG[key[0:1]]), bufs=ALL_BUFS[tag or PS_TAG[key[0:1]]])
                 for u in range(2):
                     for jj in range(2):
                         j = 2 * b + jj
@@ -93,13 +98,19 @@ def tile_gatedcrossattention_pb_t_kernel(tc, query, hr, Wu, bu, Wh, bh, out):
                             sw[:, j * 256 + u * P:j * 256 + (u + 1) * P],
                             ident[:],
                         )
-                dst = gw[:, b * 512:(b + 1) * 512].rearrange("p (r u) -> p r u", u=2)
-                srcv = bank[:].rearrange("p (u r) -> p r u", u=2)
-                if engines[b] == "S":
-                    nc.scalar.copy(out=dst, in_=srcv)
-                else:
-                    nc.vector.tensor_copy(out=dst, in_=srcv)
-            grp[key] = grouped
+                banks[(key, b)] = bank
+
+        def lay(key, b, engine):
+            tag = key[0:1] if key[0:1] != "w" else key
+            if b == 0:
+                grp[key] = work.tile([P, NT * E], BF16, name="grp_%s" % key, tag="grp_" + tag, bufs=GRP_BUFS[tag], align_bytes=64)
+            gw = grp[key][:].bitcast(F32)
+            dst = gw[:, b * 512:(b + 1) * 512].rearrange("p (r u) -> p r u", u=2)
+            srcv = banks[(key, b)][:].rearrange("p (u r) -> p r u", u=2)
+            if engine == "S":
+                nc.scalar.copy(out=dst, in_=srcv)
+            else:
+                nc.vector.tensor_copy(out=dst, in_=srcv)
 
         def quantise(key, tag):
             cw = work.tile([P, 512], U32, name="cw_%s" % key, tag="cw_" + tag, bufs=Q_BUFS[tag], align_bytes=64)
@@ -108,23 +119,21 @@ def tile_gatedcrossattention_pb_t_kernel(tc, query, hr, Wu, bu, Wh, bh, out):
             codes[key] = cw
             planes[key] = sp
 
-        def fwd(kind, g, engines):
-            if 0 <= g < NG:
-                forward("%s%d" % (kind, g), kind, engines)
-
-        def quant(kind, g):
-            if 0 <= g < NG:
-                quantise("%s%d" % (kind, g), kind)
+        def qz(key):
+            quantise(key, key[0:1] if key[0:1] != "w" else key)
 
         bias = const.tile([P, 8], F32, name="bias")
 
         def make_bias():
-            bank = psum.tile([P, 512], F32, name="tp_bias", tag="tp", bufs=TP_BUFS)
+            bank = psum.tile([P, 512], F32, name="tp_bias", tag="ht", bufs=1)
             nc.tensor.transpose(bank[:, 0:P], brow[:].bitcast(F32), ident[:])
             nc.vector.tensor_copy(out=bias[:], in_=bank[:, 0:4].bitcast(BF16))
 
-        def mx(wname, key, dst, func, bcol):
-            for t in range(NT):
+        zb = {}
+        GATE_BUFS = 2
+
+        def mx_pass(wname, key, ts):
+            for t in ts:
                 z = psum.tile([P, 512], F32, name="z_%s_%d" % (key, t), tag="z", bufs=Z_BUFS)
                 nc.tensor.matmul_mx(
                     out=z[:],
@@ -135,16 +144,18 @@ def tile_gatedcrossattention_pb_t_kernel(tc, query, hr, Wu, bu, Wh, bh, out):
                     start=True,
                     stop=True,
                 )
+                zb[(key, t)] = z
+
+        def mx_act(key, dst, func, bcol, ts):
+            for t in ts:
                 nc.scalar.activation(
-                    out=dst[:, t * RG:(t + 1) * RG], in_=z[:], func=func,
+                    out=dst[:, t * RG:(t + 1) * RG], in_=zb[(key, t)][:], func=func,
                     bias=bias[:, bcol + t:bcol + t + 1], scale=1.0,
                 )
 
-        def back(g, js):
-            if g < 0 or g >= NG:
-                return
-            if g not in o_sb:
-                o_sb[g] = rows.tile([P, NT * E], F32, name="orow%d" % g, tag="orow", bufs=3)
+        ob = {}
+
+        def back_turn(g, js):
             for j in js:
                 ot = psum.tile([P, 512], F32, name="ot_%d_%d" % (g, j), tag="ot", bufs=OT_BUFS)
                 for t in range(NT):
@@ -153,9 +164,15 @@ def tile_gatedcrossattention_pb_t_kernel(tc, query, hr, Wu, bu, Wh, bh, out):
                         cand[g][:, t * RG + j * P:t * RG + (j + 1) * P],
                         ident[:],
                     )
+                ob[(g, j)] = ot
+
+        def back_add(g, js):
+            if g not in o_sb:
+                o_sb[g] = rows.tile([P, NT * E], F32, name="orow%d" % g, tag="orow", bufs=3)
+            for j in js:
                 nc.vector.tensor_tensor(
                     out=o_sb[g][:, j * E:(j + 1) * E].rearrange("p (u m e) -> p u m e", u=2, e=2),
-                    in0=ot[:].rearrange("p (u e m) -> p u m e", u=2, e=2),
+                    in0=ob[(g, j)][:].rearrange("p (u e m) -> p u m e", u=2, e=2),
                     in1=src_sb["x%d" % g][:, j * E:(j + 1) * E].rearrange("p (u m e) -> p u m e", u=2, e=2),
                     op=ALU.add,
                 )
@@ -171,55 +188,488 @@ def tile_gatedcrossattention_pb_t_kernel(tc, query, hr, Wu, bu, Wh, bh, out):
                     out=of[g * RG:(g + 1) * RG, :].rearrange("(p j) e -> p (j e)", j=NT), in_=o_sb[g][:]
                 )
 
+        CAND_BUFS = 5
+
+        def sub_x(g, b):
+            c4 = cand[g][:].rearrange("p (u e r) -> p u e r", u=2, e=2)[:, :, :, b * 256:(b + 1) * 256]
+            xb = banks[("x%d" % g, b)][:].bitcast(BF16).rearrange("p (u r e) -> p u e r", u=2, e=2)
+            nc.vector.tensor_tensor(out=c4, in0=c4, in1=xb, op=ALU.subtract)
+
+        def mul_gate(g, engine, lo, hi):
+            eng = nc.vector if engine == "V" else nc.gpsimd
+            eng.tensor_tensor(out=cand[g][:, lo:hi], in0=gate[g][:, lo:hi], in1=cand[g][:, lo:hi], op=ALU.mult)
+
         load_w("wh", Wh)
         load_rows("h", 0)
         load_w("wu", Wu)
         load_rows("x", 0)
-        for g in range(1, 3):
-            load_rows("h", g)
-            load_rows("x", g)
-        SV = ("S", "V")
-        forward("wh", "wh", SV)
-        fwd("h", 0, SV)
-        quantise("wh", "wh")
-        quant("h", 0)
+        load_rows("h", 1)
+        load_rows("x", 1)
+        load_rows("h", 2)
+        load_rows("h", 3)
+        load_rows("x", 2)
         make_bias()
-        forward("wu", "wu", SV)
-        fwd("x", 0, SV)
-        quantise("wu", "wu")
-        quant("x", 0)
-        for g in range(1, LAG):
-            fwd("h", g, SV)
-            fwd("x", g, SV)
-            quant("h", g)
-            quant("x", g)
-        for i in range(0, NG + 1):
-            eng = ("S", "S")
-            load_rows("h", i + 3)
-            load_rows("x", i + 3)
-            live = 0 <= i < NG
-            if live:
-                cand[i] = work.tile([P, NT * RG], F32, name="cand%d" % i, tag="cand", bufs=3)
-                mx("wh", "h%d" % i, cand[i], ACT.Tanh, 4)
-                gate[i] = work.tile([P, NT * RG], F32, name="gate%d" % i, tag="gate", bufs=2)
-                mx("wu", "x%d" % i, gate[i], ACT.Sigmoid, 0)
-                c3 = cand[i][:].rearrange("p (t r) -> p t r", t=NT)
-                nc.vector.tensor_tensor(
-                    out=c3, in0=c3, in1=grp["x%d" % i][:].rearrange("p (r t) -> p t r", t=NT), op=ALU.subtract
-                )
-                split = NT * RG - (G_COLS if i > 0 else 0)
-                if split < NT * RG:
-                    nc.gpsimd.tensor_tensor(
-                        out=cand[i][:, split:], in0=gate[i][:, split:], in1=cand[i][:, split:], op=ALU.mult
-                    )
-            fwd("h", i + LAG, eng)
-            back(i - 1, (0, 1, 2))
-            fwd("x", i + LAG, eng)
-            back(i - 1, (3,))
-            if live:
-                store(i - 1)
-                nc.vector.tensor_tensor(
-                    out=cand[i][:, 0:split], in0=gate[i][:, 0:split], in1=cand[i][:, 0:split], op=ALU.mult
-                )
-            quant("h", i + LAG)
-            quant("x", i + LAG)
+        turn("wh", (0, 1,))
+        lay("wh", 0, "V")
+        lay("wh", 1, "S")
+        turn("h0", (0,))
+        lay("h0", 0, "S")
+        turn("h0", (1,))
+        qz("wh")
+        turn("wu", (0, 1,))
+        lay("wu", 0, "S")
+        lay("h0", 1, "V")
+        turn("x0", (0,))
+        qz("h0")
+        lay("wu", 1, "V")
+        turn("h1", (0,))
+        turn("x0", (1,))
+        lay("h1", 0, "V")
+        turn("h1", (1,))
+        qz("wu")
+        cand[0] = work.tile([P, NT * RG], F32, name="cand0", tag="cand", bufs=CAND_BUFS)
+        mx_pass("wh", "h0", (0, 1, 2, 3,))
+        lay("x0", 0, "S")
+        lay("h1", 1, "V")
+        qz("h1")
+        turn("h2", (0,))
+        cand[1] = work.tile([P, NT * RG], F32, name="cand1", tag="cand", bufs=CAND_BUFS)
+        mx_pass("wh", "h1", (0, 1, 2, 3,))
+        turn("h2", (1,))
+        lay("x0", 1, "V")
+        mx_act("h0", cand[0], ACT.Tanh, 4, (0, 1, 2, 3,))
+        turn("x1", (1,))
+        lay("h2", 0, "S")
+        qz("x0")
+        turn("x1", (0,))
+        mx_act("h1", cand[1], ACT.Tanh, 4, (0, 1, 2, 3,))
+        gate[0] = work.tile([P, NT * RG], F32, name="gate0", tag="gate", bufs=GATE_BUFS)
+        mx_pass("wu", "x0", (0, 1, 2, 3,))
+        sub_x(0, 0)
+        lay("x1", 0, "S")
+        sub_x(0, 1)
+        load_rows("h", 4)
+        load_rows("x", 3)
+        mx_act("x0", gate[0], ACT.Sigmoid, 0, (0, 1, 2, 3,))
+        lay("h2", 1, "V")
+        lay("x1", 1, "V")
+        turn("h3", (0,))
+        mul_gate(0, "G", 0, 1024)
+        qz("h2")
+        qz("x1")
+        lay("h3", 0, "S")
+        cand[2] = work.tile([P, NT * RG], F32, name="cand2", tag="cand", bufs=CAND_BUFS)
+        mx_pass("wh", "h2", (0, 1, 2, 3,))
+        turn("x2", (0,))
+        turn("x2", (1,))
+        sub_x(1, 1)
+        mx_act("h2", cand[2], ACT.Tanh, 4, (0, 1, 2, 3,))
+        sub_x(1, 0)
+        turn("h3", (1,))
+        gate[1] = work.tile([P, NT * RG], F32, name="gate1", tag="gate", bufs=GATE_BUFS)
+        mx_pass("wu", "x1", (0, 1, 2, 3,))
+        lay("x2", 0, "V")
+        mul_gate(0, "G", 1024, 2048)
+        lay("h3", 1, "V")
+        lay("x2", 1, "S")
+        load_rows("h", 5)
+        load_rows("x", 4)
+        mx_act("x1", gate[1], ACT.Sigmoid, 0, (0, 1, 2, 3,))
+        qz("h3")
+        back_turn(0, (0, 1,))
+        qz("x2")
+        cand[3] = work.tile([P, NT * RG], F32, name="cand3", tag="cand", bufs=CAND_BUFS)
+        mx_pass("wh", "h3", (0, 1, 2, 3,))
+        mx_act("h3", cand[3], ACT.Tanh, 4, (0, 1, 2, 3,))
+        mul_gate(1, "G", 0, 1024)
+        sub_x(2, 0)
+        turn("h4", (0,))
+        back_turn(0, (2,))
+        back_add(0, (0,))
+        turn("x3", (1,))
+        lay("h4", 0, "S")
+        sub_x(2, 1)
+        back_add(0, (1,))
+        turn("x3", (0,))
+        lay("x3", 0, "S")
+        lay("x3", 1, "V")
+        back_turn(0, (3,))
+        back_add(0, (2, 3,))
+        turn("h4", (1,))
+        mul_gate(1, "G", 1024, 2048)
+        lay("h4", 1, "S")
+        store(0)
+        qz("x3")
+        gate[2] = work.tile([P, NT * RG], F32, name="gate2", tag="gate", bufs=GATE_BUFS)
+        mx_pass("wu", "x2", (0, 1, 2, 3,))
+        qz("h4")
+        load_rows("h", 6)
+        load_rows("x", 5)
+        mx_act("x2", gate[2], ACT.Sigmoid, 0, (0, 1, 2, 3,))
+        mul_gate(2, "G", 0, 1024)
+        mul_gate(2, "G", 1024, 2048)
+        back_turn(1, (0, 1,))
+        cand[4] = work.tile([P, NT * RG], F32, name="cand4", tag="cand", bufs=CAND_BUFS)
+        mx_pass("wh", "h4", (0, 1, 2, 3,))
+        mx_act("h4", cand[4], ACT.Tanh, 4, (0, 1, 2, 3,))
+        turn("h5", (0,))
+        sub_x(3, 0)
+        turn("x4", (0,))
+        sub_x(3, 1)
+        turn("x4", (1,))
+        lay("h5", 0, "S")
+        lay("x4", 0, "S")
+        back_add(1, (0,))
+        back_turn(1, (2,))
+        back_add(1, (1,))
+        back_turn(1, (3,))
+        turn("h5", (1,))
+        lay("h5", 1, "S")
+        back_add(1, (2, 3,))
+        store(1)
+        lay("x4", 1, "V")
+        gate[3] = work.tile([P, NT * RG], F32, name="gate3", tag="gate", bufs=GATE_BUFS)
+        mx_pass("wu", "x3", (0, 1, 2, 3,))
+        qz("x4")
+        qz("h5")
+        load_rows("h", 7)
+        load_rows("x", 6)
+        mx_act("x3", gate[3], ACT.Sigmoid, 0, (0, 1, 2, 3,))
+        mul_gate(3, "G", 0, 1024)
+        mul_gate(3, "G", 1024, 2048)
+        back_turn(2, (0, 1,))
+        cand[5] = work.tile([P, NT * RG], F32, name="cand5", tag="cand", bufs=CAND_BUFS)
+        mx_pass("wh", "h5", (0, 1, 2, 3,))
+        mx_act("h5", cand[5], ACT.Tanh, 4, (0, 1, 2, 3,))
+        turn("h6", (0,))
+        sub_x(4, 0)
+        turn("x5", (0,))
+        sub_x(4, 1)
+        turn("x5", (1,))
+        lay("h6", 0, "S")
+        lay("x5", 0, "S")
+        back_add(2, (0,))
+        back_turn(2, (2,))
+        back_add(2, (1,))
+        back_turn(2, (3,))
+        turn("h6", (1,))
+        lay("h6", 1, "S")
+        back_add(2, (2, 3,))
+        store(2)
+        lay("x5", 1, "V")
+        gate[4] = work.tile([P, NT * RG], F32, name="gate4", tag="gate", bufs=GATE_BUFS)
+        mx_pass("wu", "x4", (0, 1, 2, 3,))
+        qz("x5")
+        qz("h6")
+        load_rows("h", 8)
+        load_rows("x", 7)
+        mx_act("x4", gate[4], ACT.Sigmoid, 0, (0, 1, 2, 3,))
+        mul_gate(4, "G", 0, 1024)
+        mul_gate(4, "G", 1024, 2048)
+        back_turn(3, (0, 1,))
+        cand[6] = work.tile([P, NT * RG], F32, name="cand6", tag="cand", bufs=CAND_BUFS)
+        mx_pass("wh", "h6", (0, 1, 2, 3,))
+        mx_act("h6", cand[6], ACT.Tanh, 4, (0, 1, 2, 3,))
+        turn("h7", (0,))
+        sub_x(5, 0)
+        turn("x6", (0,))
+        sub_x(5, 1)
+        turn("x6", (1,))
+        lay("h7", 0, "S")
+        lay("x6", 0, "S")
+        back_add(3, (0,))
+        back_turn(3, (2,))
+        back_add(3, (1,))
+        back_turn(3, (3,))
+        turn("h7", (1,))
+        lay("h7", 1, "S")
+        back_add(3, (2, 3,))
+        store(3)
+        lay("x6", 1, "V")
+        gate[5] = work.tile([P, NT * RG], F32, name="gate5", tag="gate", bufs=GATE_BUFS)
+        mx_pass("wu", "x5", (0, 1, 2, 3,))
+        qz("x6")
+        qz("h7")
+        load_rows("h", 9)
+        load_rows("x", 8)
+        mx_act("x5", gate[5], ACT.Sigmoid, 0, (0, 1, 2, 3,))
+        mul_gate(5, "G", 0, 1024)
+        mul_gate(5, "G", 1024, 2048)
+        back_turn(4, (0, 1,))
+        cand[7] = work.tile([P, NT * RG], F32, name="cand7", tag="cand", bufs=CAND_BUFS)
+        mx_pass("wh", "h7", (0, 1, 2, 3,))
+        mx_act("h7", cand[7], ACT.Tanh, 4, (0, 1, 2, 3,))
+        turn("h8", (0,))
+        sub_x(6, 0)
+        turn("x7", (0,))
+        sub_x(6, 1)
+        turn("x7", (1,))
+        lay("h8", 0, "S")
+        lay("x7", 0, "S")
+        back_add(4, (0,))
+        back_turn(4, (2,))
+        back_add(4, (1,))
+        back_turn(4, (3,))
+        turn("h8", (1,))
+        lay("h8", 1, "S")
+        back_add(4, (2, 3,))
+        store(4)
+        lay("x7", 1, "V")
+        gate[6] = work.tile([P, NT * RG], F32, name="gate6", tag="gate", bufs=GATE_BUFS)
+        mx_pass("wu", "x6", (0, 1, 2, 3,))
+        qz("x7")
+        qz("h8")
+        load_rows("h", 10)
+        load_rows("x", 9)
+        mx_act("x6", gate[6], ACT.Sigmoid, 0, (0, 1, 2, 3,))
+        mul_gate(6, "G", 0, 1024)
+        mul_gate(6, "G", 1024, 2048)
+        back_turn(5, (0, 1,))
+        cand[8] = work.tile([P, NT * RG], F32, name="cand8", tag="cand", bufs=CAND_BUFS)
+        mx_pass("wh", "h8", (0, 1, 2, 3,))
+        mx_act("h8", cand[8], ACT.Tanh, 4, (0, 1, 2, 3,))
+        turn("h9", (0,))
+        sub_x(7, 0)
+        turn("x8", (0,))
+        sub_x(7, 1)
+        turn("x8", (1,))
+        lay("h9", 0, "S")
+        lay("x8", 0, "S")
+        back_add(5, (0,))
+        back_turn(5, (2,))
+        back_add(5, (1,))
+        back_turn(5, (3,))
+        turn("h9", (1,))
+        lay("h9", 1, "S")
+        back_add(5, (2, 3,))
+        store(5)
+        lay("x8", 1, "V")
+        gate[7] = work.tile([P, NT * RG], F32, name="gate7", tag="gate", bufs=GATE_BUFS)
+        mx_pass("wu", "x7", (0, 1, 2, 3,))
+        qz("x8")
+        qz("h9")
+        load_rows("h", 11)
+        load_rows("x", 10)
+        mx_act("x7", gate[7], ACT.Sigmoid, 0, (0, 1, 2, 3,))
+        mul_gate(7, "G", 0, 1024)
+        mul_gate(7, "G", 1024, 2048)
+        back_turn(6, (0, 1,))
+        cand[9] = work.tile([P, NT * RG], F32, name="cand9", tag="cand", bufs=CAND_BUFS)
+        mx_pass("wh", "h9", (0, 1, 2, 3,))
+        mx_act("h9", cand[9], ACT.Tanh, 4, (0, 1, 2, 3,))
+        turn("h10", (0,))
+        sub_x(8, 0)
+        turn("x9", (0,))
+        sub_x(8, 1)
+        turn("x9", (1,))
+        lay("h10", 0, "S")
+        lay("x9", 0, "S")
+        back_add(6, (0,))
+        back_turn(6, (2,))
+        back_add(6, (1,))
+        back_turn(6, (3,))
+        turn("h10", (1,))
+        lay("h10", 1, "S")
+        back_add(6, (2, 3,))
+        store(6)
+        lay("x9", 1, "V")
+        gate[8] = work.tile([P, NT * RG], F32, name="gate8", tag="gate", bufs=GATE_BUFS)
+        mx_pass("wu", "x8", (0, 1, 2, 3,))
+        qz("x9")
+        qz("h10")
+        load_rows("h", 12)
+        load_rows("x", 11)
+        mx_act("x8", gate[8], ACT.Sigmoid, 0, (0, 1, 2, 3,))
+        mul_gate(8, "G", 0, 1024)
+        mul_gate(8, "G", 1024, 2048)
+        back_turn(7, (0, 1,))
+        cand[10] = work.tile([P, NT * RG], F32, name="cand10", tag="cand", bufs=CAND_BUFS)
+        mx_pass("wh", "h10", (0, 1, 2, 3,))
+        mx_act("h10", cand[10], ACT.Tanh, 4, (0, 1, 2, 3,))
+        turn("h11", (0,))
+        sub_x(9, 0)
+        turn("x10", (0,))
+        sub_x(9, 1)
+        turn("x10", (1,))
+        lay("h11", 0, "S")
+        lay("x10", 0, "S")
+        back_add(7, (0,))
+        back_turn(7, (2,))
+        back_add(7, (1,))
+        back_turn(7, (3,))
+        turn("h11", (1,))
+        lay("h11", 1, "S")
+        back_add(7, (2, 3,))
+        store(7)
+        lay("x10", 1, "V")
+        gate[9] = work.tile([P, NT * RG], F32, name="gate9", tag="gate", bufs=GATE_BUFS)
+        mx_pass("wu", "x9", (0, 1, 2, 3,))
+        qz("x10")
+        qz("h11")
+        load_rows("h", 13)
+        load_rows("x", 12)
+        mx_act("x9", gate[9], ACT.Sigmoid, 0, (0, 1, 2, 3,))
+        mul_gate(9, "G", 0, 1024)
+        mul_gate(9, "G", 1024, 2048)
+        back_turn(8, (0, 1,))
+        cand[11] = work.tile([P, NT * RG], F32, name="cand11", tag="cand", bufs=CAND_BUFS)
+        mx_pass("wh", "h11", (0, 1, 2, 3,))
+        mx_act("h11", cand[11], ACT.Tanh, 4, (0, 1, 2, 3,))
+        turn("h12", (0,))
+        sub_x(10, 0)
+        turn("x11", (0,))
+        sub_x(10, 1)
+        turn("x11", (1,))
+        lay("h12", 0, "S")
+        lay("x11", 0, "S")
+        back_add(8, (0,))
+        back_turn(8, (2,))
+        back_add(8, (1,))
+        back_turn(8, (3,))
+        turn("h12", (1,))
+        lay("h12", 1, "S")
+        back_add(8, (2, 3,))
+        store(8)
+        lay("x11", 1, "V")
+        gate[10] = work.tile([P, NT * RG], F32, name="gate10", tag="gate", bufs=GATE_BUFS)
+        mx_pass("wu", "x10", (0, 1, 2, 3,))
+        qz("x11")
+        qz("h12")
+        load_rows("h", 14)
+        load_rows("x", 13)
+        mx_act("x10", gate[10], ACT.Sigmoid, 0, (0, 1, 2, 3,))
+        mul_gate(10, "G", 0, 1024)
+        mul_gate(10, "G", 1024, 2048)
+        back_turn(9, (0, 1,))
+        cand[12] = work.tile([P, NT * RG], F32, name="cand12", tag="cand", bufs=CAND_BUFS)
+        mx_pass("wh", "h12", (0, 1, 2, 3,))
+        mx_act("h12", cand[12], ACT.Tanh, 4, (0, 1, 2, 3,))
+        turn("h13", (0,))
+        sub_x(11, 0)
+        turn("x12", (0,))
+        sub_x(11, 1)
+        turn("x12", (1,))
+        lay("h13", 0, "S")
+        lay("x12", 0, "S")
+        back_add(9, (0,))
+        back_turn(9, (2,))
+        back_add(9, (1,))
+        back_turn(9, (3,))
+        turn("h13", (1,))
+        lay("h13", 1, "S")
+        back_add(9, (2, 3,))
+        store(9)
+        lay("x12", 1, "V")
+        gate[11] = work.tile([P, NT * RG], F32, name="gate11", tag="gate", bufs=GATE_BUFS)
+        mx_pass("wu", "x11", (0, 1, 2, 3,))
+        qz("x12")
+        qz("h13")
+        load_rows("h", 15)
+        load_rows("x", 14)
+        mx_act("x11", gate[11], ACT.Sigmoid, 0, (0, 1, 2, 3,))
+        mul_gate(11, "G", 0, 1024)
+        mul_gate(11, "G", 1024, 2048)
+        back_turn(10, (0, 1,))
+        cand[13] = work.tile([P, NT * RG], F32, name="cand13", tag="cand", bufs=CAND_BUFS)
+        mx_pass("wh", "h13", (0, 1, 2, 3,))
+        mx_act("h13", cand[13], ACT.Tanh, 4, (0, 1, 2, 3,))
+        turn("h14", (0,))
+        sub_x(12, 0)
+        turn("x13", (0,))
+        sub_x(12, 1)
+        turn("x13", (1,))
+        lay("h14", 0, "S")
+        lay("x13", 0, "S")
+        back_add(10, (0,))
+        back_turn(10, (2,))
+        back_add(10, (1,))
+        back_turn(10, (3,))
+        turn("h14", (1,))
+        lay("h14", 1, "S")
+        back_add(10, (2, 3,))
+        store(10)
+        lay("x13", 1, "V")
+        gate[12] = work.tile([P, NT * RG], F32, name="gate12", tag="gate", bufs=GATE_BUFS)
+        mx_pass("wu", "x12", (0, 1, 2, 3,))
+        qz("x13")
+        qz("h14")
+        load_rows("x", 15)
+        mx_act("x12", gate[12], ACT.Sigmoid, 0, (0, 1, 2, 3,))
+        mul_gate(12, "G", 0, 1024)
+        mul_gate(12, "G", 1024, 2048)
+        back_turn(11, (0, 1,))
+        cand[14] = work.tile([P, NT * RG], F32, name="cand14", tag="cand", bufs=CAND_BUFS)
+        mx_pass("wh", "h14", (0, 1, 2, 3,))
+        mx_act("h14", cand[14], ACT.Tanh, 4, (0, 1, 2, 3,))
+        turn("h15", (0,))
+        sub_x(13, 0)
+        turn("x14", (0,))
+        sub_x(13, 1)
+        turn("x14", (1,))
+        lay("h15", 0, "S")
+        lay("x14", 0, "S")
+        back_add(11, (0,))
+        back_turn(11, (2,))
+        back_add(11, (1,))
+        back_turn(11, (3,))
+        turn("h15", (1,))
+        lay("h15", 1, "S")
+        back_add(11, (2, 3,))
+        store(11)
+        lay("x14", 1, "V")
+        gate[13] = work.tile([P, NT * RG], F32, name="gate13", tag="gate", bufs=GATE_BUFS)
+        mx_pass("wu", "x13", (0, 1, 2, 3,))
+        qz("x14")
+        qz("h15")
+        mx_act("x13", gate[13], ACT.Sigmoid, 0, (0, 1, 2, 3,))
+        sub_x(14, 0)
+        back_turn(12, (0, 1,))
+        sub_x(14, 1)
+        mul_gate(13, "G", 0, 1024)
+        cand[15] = work.tile([P, NT * RG], F32, name="cand15", tag="cand", bufs=CAND_BUFS)
+        mx_pass("wh", "h15", (0, 1, 2, 3,))
+        turn("x15", (0,))
+        mx_act("h15", cand[15], ACT.Tanh, 4, (0, 1, 2, 3,))
+        turn("x15", (1,))
+        back_turn(12, (2,))
+        gate[14] = work.tile([P, NT * RG], F32, name="gate14", tag="gate", bufs=GATE_BUFS)
+        mx_pass("wu", "x14", (0, 1, 2, 3,))
+        mul_gate(13, "G", 1024, 2048)
+        lay("x15", 0, "S")
+        mx_act("x14", gate[14], ACT.Sigmoid, 0, (0, 1, 2, 3,))
+        back_add(12, (0,))
+        back_turn(12, (3,))
+        back_add(12, (1,))
+        lay("x15", 1, "V")
+        qz("x15")
+        back_add(12, (2, 3,))
+        sub_x(15, 1)
+        mul_gate(14, "G", 0, 1024)
+        back_turn(13, (0, 1,))
+        back_add(13, (0,))
+        store(12)
+        sub_x(15, 0)
+        gate[15] = work.tile([P, NT * RG], F32, name="gate15", tag="gate", bufs=GATE_BUFS)
+        mx_pass("wu", "x15", (0, 1, 2, 3,))
+        back_turn(13, (2,))
+        back_turn(13, (3,))
+        back_add(13, (1,))
+        mul_gate(14, "G", 1024, 2048)
+        back_turn(14, (0, 1,))
+        back_add(13, (2, 3,))
+        mx_act("x15", gate[15], ACT.Sigmoid, 0, (0, 1, 2, 3,))
+        back_add(14, (0,))
+        mul_gate(15, "G", 0, 1024)
+        back_turn(14, (2,))
+        back_turn(14, (3,))
+        back_add(14, (1,))
+        store(13)
+        mul_gate(15, "G", 1024, 2048)
+        back_add(14, (2, 3,))
+        back_turn(15, (0, 1,))
+        back_turn(15, (2,))
+        back_turn(15, (3,))
+        store(14)
+        back_add(15, (0,))
+        back_add(15, (1,))
+        back_add(15, (2, 3,))

@@ -1,8 +1,6 @@
 from contextlib import ExitStack
 
-import concourse.bass as bass
 import concourse.mybir as mybir
-import concourse.tile as tile
 from concourse.masks import make_identity
 
 F32 = mybir.dt.float32
@@ -15,661 +13,267 @@ ALU = mybir.AluOpType
 
 P = 128
 E = 512
-ROWS = 8192
-RG = 512
-NG = ROWS // RG
-NT = 4
+ROWS = 2048 * 4
+GROUP = 512
+GROUPS = ROWS // GROUP
+TILES = 4
+HALF = GROUP // 2
 FLOPS = 2 * 2 * ROWS * E * E
 
-G_COLS = 0
-LAG = 3
-Z_BUFS = 3
-OT_BUFS = 2
-TP_BUFS = 2
+BANKS = {"xT": 2, "hT": 1, "mx": 3, "back": 2}
+WEIGHTS = {"h": "Wh", "x": "Wu"}
+ROW_SLOTS = {"h": 4, "x": 6}
+RESULT_SLOTS = {"h": 5, "x": 2}
+OUT_SLOTS = 3
+STREAM_SLOTS = 2
 
 
 def tile_gatedcrossattention_pb_t_kernel(tc, query, hr, Wu, bu, Wh, bh, out):
     nc = tc.nc
-    xf = query.rearrange("t b e -> (t b) e")
-    hf = hr.rearrange("t b e -> (t b) e")
-    of = out.rearrange("t b e -> (t b) e")
+    dram = {"x": query.rearrange("t b e -> (t b) e"), "h": hr.rearrange("t b e -> (t b) e")}
+    out_rows = out.rearrange("t b e -> (t b) e")
 
     with ExitStack() as ctx:
         const = ctx.enter_context(tc.tile_pool(name="const", bufs=1))
-        rows = ctx.enter_context(tc.tile_pool(name="rows", bufs=3))
-        work = ctx.enter_context(tc.tile_pool(name="work", bufs=3))
-        psum = ctx.enter_context(tc.psum_pool(name="psum", bufs=2))
+        rows = ctx.enter_context(tc.tile_pool(name="rows", bufs=1))
+        work = ctx.enter_context(tc.tile_pool(name="work", bufs=1))
+        psum = ctx.enter_context(tc.psum_pool(name="psum", bufs=1))
         ctx.enter_context(tc.manual_schedule())
 
-        brow = const.tile([P, 2 * P], BF16, name="brow")
-        nc.vector.memset(brow[:], 0.0)
-        zero1 = const.tile([P, 1], F32, name="zero1")
-        nc.vector.memset(zero1[:], 0.0)
-        nc.sync.dma_start(out=brow[0:2, :], in_=bu.rearrange("(u c) -> u c", u=2))
-        nc.sync.dma_start(out=brow[2:4, :], in_=bh.rearrange("(u c) -> u c", u=2))
-        warm = const.tile([P, 1], F32, name="warm")
-        nc.scalar.activation(out=warm[:], in_=zero1[:], func=ACT.Sigmoid)
-        ident = const.tile([P, P], F32, name="ident")
-        make_identity(nc, ident[:])
-
-        src_sb = {}
-        grp = {}
-        codes = {}
-        planes = {}
-        gate = {}
-        cand = {}
-        o_sb = {}
-
-        def load_w(name, w):
-            wt = const.tile([P, NT * E], BF16, name="row_" + name)
-            nc.sync.dma_start(
-                out=wt[:].rearrange("m (u e k) -> m u e k", u=2, e=2),
-                in_=w.rearrange("(u m e) k -> m u e k", u=2, e=2),
-            )
-            src_sb[name] = wt
-
-        def load_rows(kind, g):
-            if g < 0 or g >= NG:
-                return
-            srcf = hf if kind == "h" else xf
-            rt = rows.tile([P, NT * E], BF16, name="%srow%d" % (kind, g), tag=kind + "row", bufs=(4 if kind == "h" else 7))
-            nc.sync.dma_start(out=rt[:], in_=srcf[g * RG:(g + 1) * RG, :].rearrange("(p j) e -> p (j e)", j=NT))
-            src_sb["%s%d" % (kind, g)] = rt
-
-        GRP_BUFS = {"wh": 1, "wu": 1, "h": 2, "x": 2}
-        Q_BUFS = {"wh": 1, "wu": 1, "h": LAG + 1, "x": LAG + 1}
-
+        loaded = {}
         banks = {}
+        grouped = {}
+        codes = {}
+        scales = {}
+        sums = {}
+        result = {}
+        turned = {}
+        blended = {}
 
-        PS_TAG = {"w": "xt", "x": "xt", "h": "ht"}
-        PS_BUFS = {"w": 2, "x": 2, "h": 1}
+        def live(g):
+            return 0 <= g < GROUPS
 
-        ALL_BUFS = {"xt": 2, "ht": 1, "z": Z_BUFS, "ot": OT_BUFS}
+        def slots(name):
+            return STREAM_SLOTS if name in WEIGHTS else 1
 
-        def turn(key, bs=(0, 1), tag=None):
-            sw = src_sb[key][:].bitcast(F32)
-            for b in bs:
-                bank = psum.tile([P, 512], F32, name="tp_%s_%d" % (key, b), tag=(tag or PS_TAG[key[0:1]]), bufs=ALL_BUFS[tag or PS_TAG[key[0:1]]])
-                for u in range(2):
-                    for jj in range(2):
-                        j = 2 * b + jj
+        def group_view(flat, g):
+            return flat[g * GROUP:(g + 1) * GROUP, :].rearrange("(p j) e -> p j e", j=TILES)
+
+
+        def load_rows(name, g):
+            if live(g):
+                tile_ = rows.tile([P, TILES * E], BF16, name="rows_%s%d" % (name, g), tag="rows_" + name, bufs=ROW_SLOTS[name])
+                nc.sync.dma_start(out=tile_[:].rearrange("p (j e) -> p j e", j=TILES), in_=group_view(dram[name], g))
+                loaded[(name, g)] = tile_
+
+        def load_weights(name, w):
+            tile_ = const.tile([P, TILES * E], BF16, name="rows_" + name)
+            nc.sync.dma_start(
+                out=tile_[:].rearrange("m (a e k) -> m a e k", a=2, e=2),
+                in_=w.rearrange("(a m e) k -> m a e k", a=2, e=2),
+            )
+            loaded[(name, 0)] = tile_
+
+        def turn(name, g, halves, role):
+            if not live(g):
+                return
+            words = loaded[(name, g)][:].bitcast(F32)
+            for half in halves:
+                bank = psum.tile([P, GROUP], F32, name="T_%s%d_%d" % (name, g, half), tag=role, bufs=BANKS[role])
+                for a in range(2):
+                    for k in range(2):
+                        j = 2 * half + k
                         nc.tensor.transpose(
-                            bank[:, u * 256 + jj * P:u * 256 + (jj + 1) * P],
-                            sw[:, j * 256 + u * P:j * 256 + (u + 1) * P],
-                            ident[:],
+                            bank[:, a * HALF + k * P:a * HALF + (k + 1) * P],
+                            words[:, j * 256 + a * P:j * 256 + (a + 1) * P],
+                            identity[:],
                         )
-                banks[(key, b)] = bank
+                banks[(name, g, half)] = bank
 
-        def lay(key, b, engine):
-            tag = key[0:1] if key[0:1] != "w" else key
-            if b == 0:
-                grp[key] = work.tile([P, NT * E], BF16, name="grp_%s" % key, tag="grp_" + tag, bufs=GRP_BUFS[tag], align_bytes=64)
-            gw = grp[key][:].bitcast(F32)
-            dst = gw[:, b * 512:(b + 1) * 512].rearrange("p (r u) -> p r u", u=2)
-            srcv = banks[(key, b)][:].rearrange("p (u r) -> p r u", u=2)
-            if engine == "S":
-                nc.scalar.copy(out=dst, in_=srcv)
-            else:
-                nc.vector.tensor_copy(out=dst, in_=srcv)
+        def lay(name, g, half, engine):
+            if not live(g):
+                return
+            if half == 0:
+                grouped[(name, g)] = work.tile(
+                    [P, TILES * GROUP], BF16, name="grouped_%s%d" % (name, g), tag="grouped_" + name, bufs=slots(name), align_bytes=64
+                )
+            dst = grouped[(name, g)][:].bitcast(F32)[:, half * GROUP:(half + 1) * GROUP]
+            engine(out=dst.rearrange("p (r a) -> p r a", a=2), in_=banks[(name, g, half)][:].rearrange("p (a r) -> p r a", a=2))
 
-        def quantise(key, tag):
-            cw = work.tile([P, 512], U32, name="cw_%s" % key, tag="cw_" + tag, bufs=Q_BUFS[tag], align_bytes=64)
-            sp = work.tile([P, 512], U8, name="sp_%s" % key, tag="sp_" + tag, bufs=Q_BUFS[tag], align_bytes=64)
-            nc.vector.quantize_mx(out=cw[:].bitcast(FP8X4), scales=sp[:], in_=grp[key][:])
-            codes[key] = cw
-            planes[key] = sp
+        def quantise(name, g):
+            if live(g):
+                words = work.tile([P, GROUP], U32, name="codes_%s%d" % (name, g), tag="codes_" + name, bufs=slots(name), align_bytes=64)
+                plane = work.tile([P, GROUP], U8, name="scales_%s%d" % (name, g), tag="scales_" + name, bufs=slots(name), align_bytes=64)
+                nc.vector.quantize_mx(out=words[:].bitcast(FP8X4), scales=plane[:], in_=grouped[(name, g)][:])
+                codes[(name, g)] = words
+                scales[(name, g)] = plane
 
-        def qz(key):
-            quantise(key, key[0:1] if key[0:1] != "w" else key)
-
-        bias = const.tile([P, 8], F32, name="bias")
-
-        def make_bias():
-            bank = psum.tile([P, 512], F32, name="tp_bias", tag="ht", bufs=1)
-            nc.tensor.transpose(bank[:, 0:P], brow[:].bitcast(F32), ident[:])
-            nc.vector.tensor_copy(out=bias[:], in_=bank[:, 0:4].bitcast(BF16))
-
-        zb = {}
-        GATE_BUFS = 2
-
-        def mx_pass(wname, key, ts):
-            for t in ts:
-                z = psum.tile([P, 512], F32, name="z_%s_%d" % (key, t), tag="z", bufs=Z_BUFS)
+        def passes(name, g):
+            if not live(g):
+                return
+            w = (WEIGHTS[name], 0)
+            result[(name, g)] = work.tile(
+                [P, TILES * GROUP], F32, name="result_%s%d" % (name, g), tag="result_" + name, bufs=RESULT_SLOTS[name]
+            )
+            for t in range(TILES):
+                bank = psum.tile([P, GROUP], F32, name="mx_%s%d_%d" % (name, g, t), tag="mx", bufs=BANKS["mx"])
                 nc.tensor.matmul_mx(
-                    out=z[:],
-                    lhsT=codes[wname][:, t * P:(t + 1) * P].bitcast(FP8X4),
-                    lhsT_scale=planes[wname][:, t * P:(t + 1) * P],
-                    rhs=codes[key][:].bitcast(FP8X4),
-                    rhs_scale=planes[key][:],
+                    out=bank[:],
+                    lhsT=codes[w][:, t * P:(t + 1) * P].bitcast(FP8X4),
+                    lhsT_scale=scales[w][:, t * P:(t + 1) * P],
+                    rhs=codes[(name, g)][:].bitcast(FP8X4),
+                    rhs_scale=scales[(name, g)][:],
                     start=True,
                     stop=True,
                 )
-                zb[(key, t)] = z
+                sums[(name, g, t)] = bank
 
-        def mx_act(key, dst, func, bcol, ts):
-            for t in ts:
-                nc.scalar.activation(
-                    out=dst[:, t * RG:(t + 1) * RG], in_=zb[(key, t)][:], func=func,
-                    bias=bias[:, bcol + t:bcol + t + 1], scale=1.0,
-                )
-
-        ob = {}
-
-        def back_turn(g, js):
-            for j in js:
-                ot = psum.tile([P, 512], F32, name="ot_%d_%d" % (g, j), tag="ot", bufs=OT_BUFS)
-                for t in range(NT):
-                    nc.tensor.transpose(
-                        ot[:, t * P:(t + 1) * P],
-                        cand[g][:, t * RG + j * P:t * RG + (j + 1) * P],
-                        ident[:],
+        def activate(name, g):
+            if live(g):
+                func, column = (ACT.Tanh, TILES) if name == "h" else (ACT.Sigmoid, 0)
+                for t in range(TILES):
+                    nc.scalar.activation(
+                        out=result[(name, g)][:, t * GROUP:(t + 1) * GROUP], in_=sums[(name, g, t)][:], func=func,
+                        bias=bias[:, column + t:column + t + 1], scale=1.0,
                     )
-                ob[(g, j)] = ot
 
-        def back_add(g, js):
-            if g not in o_sb:
-                o_sb[g] = rows.tile([P, NT * E], F32, name="orow%d" % g, tag="orow", bufs=3)
-            for j in js:
-                nc.vector.tensor_tensor(
-                    out=o_sb[g][:, j * E:(j + 1) * E].rearrange("p (u m e) -> p u m e", u=2, e=2),
-                    in0=ob[(g, j)][:].rearrange("p (u e m) -> p u m e", u=2, e=2),
-                    in1=src_sb["x%d" % g][:, j * E:(j + 1) * E].rearrange("p (u m e) -> p u m e", u=2, e=2),
-                    op=ALU.add,
-                )
-                if g == NG - 1:
-                    nc.sync.dma_start(
-                        out=of[g * RG:(g + 1) * RG, :].rearrange("(p j) e -> p j e", j=NT)[:, j, :],
-                        in_=o_sb[g][:, j * E:(j + 1) * E],
-                    )
+        def subtract_query(g, half):
+            if live(g):
+                c = result[("h", g)][:].rearrange("p (a e r) -> p a e r", a=2, e=2)[:, :, :, half * HALF:(half + 1) * HALF]
+                x_t = banks[("x", g, half)][:].bitcast(BF16).rearrange("p (a r e) -> p a e r", a=2, e=2)
+                nc.vector.tensor_tensor(out=c, in0=c, in1=x_t, op=ALU.subtract)
+
+        def multiply_gate(g):
+            if not live(g):
+                return
+            d = result[("h", g)][:].rearrange("p (t r) -> p t r", t=TILES)
+            u = result[("x", g)][:].rearrange("p (t r) -> p t r", t=TILES)
+            if g < GROUPS - 1:
+                for t in (0, 2):
+                    nc.gpsimd.tensor_tensor(out=d[:, t:t + 2, :], in0=u[:, t:t + 2, :], in1=d[:, t:t + 2, :], op=ALU.mult)
+            else:
+                for j in range(TILES):
+                    cut = slice(j * P, (j + 1) * P)
+                    nc.gpsimd.tensor_tensor(out=d[:, :, cut], in0=u[:, :, cut], in1=d[:, :, cut], op=ALU.mult)
+
+        def turn_back(g, row_tiles):
+            if live(g):
+                for j in row_tiles:
+                    bank = psum.tile([P, E], F32, name="back_%d_%d" % (g, j), tag="back", bufs=BANKS["back"])
+                    for t in range(TILES):
+                        nc.tensor.transpose(
+                            bank[:, t * P:(t + 1) * P], result[("h", g)][:, t * GROUP + j * P:t * GROUP + (j + 1) * P], identity[:]
+                        )
+                    turned[(g, j)] = bank
+
+        def add_query(g, j):
+            if not live(g):
+                return
+            if j == 0:
+                blended[g] = rows.tile([P, TILES * E], F32, name="out_%d" % g, tag="out", bufs=OUT_SLOTS)
+            cut = slice(j * E, (j + 1) * E)
+            nc.vector.tensor_tensor(
+                out=blended[g][:, cut].rearrange("p (a m e) -> p a m e", a=2, e=2),
+                in0=turned[(g, j)][:].rearrange("p (a e m) -> p a m e", a=2, e=2),
+                in1=loaded[("x", g)][:, cut].rearrange("p (a m e) -> p a m e", a=2, e=2),
+                op=ALU.add,
+            )
+            if g == GROUPS - 1:
+                nc.sync.dma_start(out=group_view(out_rows, g)[:, j, :], in_=blended[g][:, cut])
 
         def store(g):
-            if 0 <= g < NG:
-                nc.sync.dma_start(
-                    out=of[g * RG:(g + 1) * RG, :].rearrange("(p j) e -> p (j e)", j=NT), in_=o_sb[g][:]
-                )
+            if 0 <= g < GROUPS - 1:
+                nc.sync.dma_start(out=group_view(out_rows, g), in_=blended[g][:].rearrange("p (j e) -> p j e", j=TILES))
 
-        CAND_BUFS = 5
 
-        def sub_x(g, b):
-            c4 = cand[g][:].rearrange("p (u e r) -> p u e r", u=2, e=2)[:, :, :, b * 256:(b + 1) * 256]
-            xb = banks[("x%d" % g, b)][:].bitcast(BF16).rearrange("p (u r e) -> p u e r", u=2, e=2)
-            nc.vector.tensor_tensor(out=c4, in0=c4, in1=xb, op=ALU.subtract)
+        bias_rows = const.tile([P, 2 * P], BF16, name="bias_rows")
+        nc.vector.memset(bias_rows[:], 0.0)
+        zero = const.tile([P, 1], F32, name="zero")
+        nc.vector.memset(zero[:], 0.0)
+        nc.sync.dma_start(out=bias_rows[0:2, :], in_=bu.rearrange("(a c) -> a c", a=2))
+        nc.sync.dma_start(out=bias_rows[2:4, :], in_=bh.rearrange("(a c) -> a c", a=2))
+        warm = const.tile([P, 1], F32, name="warm")
+        nc.scalar.activation(out=warm[:], in_=zero[:], func=ACT.Sigmoid)
+        identity = const.tile([P, P], F32, name="identity")
+        make_identity(nc, identity[:])
+        bias = const.tile([P, 2 * TILES], F32, name="bias")
 
-        def mul_gate(g, engine, lo, hi):
-            eng = nc.vector if engine == "V" else nc.gpsimd
-            eng.tensor_tensor(out=cand[g][:, lo:hi], in0=gate[g][:, lo:hi], in1=cand[g][:, lo:hi], op=ALU.mult)
+        scalar_copy = nc.scalar.copy
+        vector_copy = nc.vector.tensor_copy
 
-        load_w("wh", Wh)
+        load_weights("Wh", Wh)
         load_rows("h", 0)
-        load_w("wu", Wu)
-        load_rows("x", 0)
+        load_weights("Wu", Wu)
         load_rows("h", 1)
+        load_rows("x", 0)
         load_rows("x", 1)
         load_rows("h", 2)
         load_rows("h", 3)
         load_rows("x", 2)
-        make_bias()
-        turn("wh", (0, 1,))
-        lay("wh", 0, "V")
-        lay("wh", 1, "S")
-        turn("h0", (0,))
-        lay("h0", 0, "S")
-        turn("h0", (1,))
-        qz("wh")
-        turn("wu", (0, 1,))
-        lay("wu", 0, "S")
-        lay("h0", 1, "V")
-        turn("x0", (0,))
-        qz("h0")
-        lay("wu", 1, "V")
-        turn("h1", (0,))
-        turn("x0", (1,))
-        lay("h1", 0, "V")
-        turn("h1", (1,))
-        qz("wu")
-        cand[0] = work.tile([P, NT * RG], F32, name="cand0", tag="cand", bufs=CAND_BUFS)
-        mx_pass("wh", "h0", (0, 1, 2, 3,))
-        lay("x0", 0, "S")
-        lay("h1", 1, "V")
-        qz("h1")
-        turn("h2", (0,))
-        cand[1] = work.tile([P, NT * RG], F32, name="cand1", tag="cand", bufs=CAND_BUFS)
-        mx_pass("wh", "h1", (0, 1, 2, 3,))
-        turn("h2", (1,))
-        lay("x0", 1, "V")
-        mx_act("h0", cand[0], ACT.Tanh, 4, (0, 1, 2, 3,))
-        turn("x1", (1,))
-        lay("h2", 0, "S")
-        qz("x0")
-        turn("x1", (0,))
-        mx_act("h1", cand[1], ACT.Tanh, 4, (0, 1, 2, 3,))
-        gate[0] = work.tile([P, NT * RG], F32, name="gate0", tag="gate", bufs=GATE_BUFS)
-        mx_pass("wu", "x0", (0, 1, 2, 3,))
-        sub_x(0, 0)
-        lay("x1", 0, "S")
-        sub_x(0, 1)
-        load_rows("h", 4)
-        load_rows("x", 3)
-        mx_act("x0", gate[0], ACT.Sigmoid, 0, (0, 1, 2, 3,))
-        lay("h2", 1, "V")
-        lay("x1", 1, "V")
-        turn("h3", (0,))
-        mul_gate(0, "G", 0, 1024)
-        qz("h2")
-        qz("x1")
-        lay("h3", 0, "S")
-        cand[2] = work.tile([P, NT * RG], F32, name="cand2", tag="cand", bufs=CAND_BUFS)
-        mx_pass("wh", "h2", (0, 1, 2, 3,))
-        turn("x2", (0,))
-        turn("x2", (1,))
-        sub_x(1, 1)
-        mx_act("h2", cand[2], ACT.Tanh, 4, (0, 1, 2, 3,))
-        sub_x(1, 0)
-        turn("h3", (1,))
-        gate[1] = work.tile([P, NT * RG], F32, name="gate1", tag="gate", bufs=GATE_BUFS)
-        mx_pass("wu", "x1", (0, 1, 2, 3,))
-        lay("x2", 0, "V")
-        mul_gate(0, "G", 1024, 2048)
-        lay("h3", 1, "V")
-        lay("x2", 1, "S")
-        load_rows("h", 5)
-        load_rows("x", 4)
-        mx_act("x1", gate[1], ACT.Sigmoid, 0, (0, 1, 2, 3,))
-        qz("h3")
-        back_turn(0, (0, 1,))
-        qz("x2")
-        cand[3] = work.tile([P, NT * RG], F32, name="cand3", tag="cand", bufs=CAND_BUFS)
-        mx_pass("wh", "h3", (0, 1, 2, 3,))
-        mx_act("h3", cand[3], ACT.Tanh, 4, (0, 1, 2, 3,))
-        mul_gate(1, "G", 0, 1024)
-        sub_x(2, 0)
-        turn("h4", (0,))
-        back_turn(0, (2,))
-        back_add(0, (0,))
-        turn("x3", (1,))
-        lay("h4", 0, "S")
-        sub_x(2, 1)
-        back_add(0, (1,))
-        turn("x3", (0,))
-        lay("x3", 0, "S")
-        lay("x3", 1, "V")
-        back_turn(0, (3,))
-        back_add(0, (2, 3,))
-        turn("h4", (1,))
-        mul_gate(1, "G", 1024, 2048)
-        lay("h4", 1, "S")
-        store(0)
-        qz("x3")
-        gate[2] = work.tile([P, NT * RG], F32, name="gate2", tag="gate", bufs=GATE_BUFS)
-        mx_pass("wu", "x2", (0, 1, 2, 3,))
-        qz("h4")
-        load_rows("h", 6)
-        load_rows("x", 5)
-        mx_act("x2", gate[2], ACT.Sigmoid, 0, (0, 1, 2, 3,))
-        mul_gate(2, "G", 0, 1024)
-        mul_gate(2, "G", 1024, 2048)
-        back_turn(1, (0, 1,))
-        cand[4] = work.tile([P, NT * RG], F32, name="cand4", tag="cand", bufs=CAND_BUFS)
-        mx_pass("wh", "h4", (0, 1, 2, 3,))
-        mx_act("h4", cand[4], ACT.Tanh, 4, (0, 1, 2, 3,))
-        turn("h5", (0,))
-        sub_x(3, 0)
-        turn("x4", (0,))
-        sub_x(3, 1)
-        turn("x4", (1,))
-        lay("h5", 0, "S")
-        lay("x4", 0, "S")
-        back_add(1, (0,))
-        back_turn(1, (2,))
-        back_add(1, (1,))
-        back_turn(1, (3,))
-        turn("h5", (1,))
-        lay("h5", 1, "S")
-        back_add(1, (2, 3,))
-        store(1)
-        lay("x4", 1, "V")
-        gate[3] = work.tile([P, NT * RG], F32, name="gate3", tag="gate", bufs=GATE_BUFS)
-        mx_pass("wu", "x3", (0, 1, 2, 3,))
-        qz("x4")
-        qz("h5")
-        load_rows("h", 7)
-        load_rows("x", 6)
-        mx_act("x3", gate[3], ACT.Sigmoid, 0, (0, 1, 2, 3,))
-        mul_gate(3, "G", 0, 1024)
-        mul_gate(3, "G", 1024, 2048)
-        back_turn(2, (0, 1,))
-        cand[5] = work.tile([P, NT * RG], F32, name="cand5", tag="cand", bufs=CAND_BUFS)
-        mx_pass("wh", "h5", (0, 1, 2, 3,))
-        mx_act("h5", cand[5], ACT.Tanh, 4, (0, 1, 2, 3,))
-        turn("h6", (0,))
-        sub_x(4, 0)
-        turn("x5", (0,))
-        sub_x(4, 1)
-        turn("x5", (1,))
-        lay("h6", 0, "S")
-        lay("x5", 0, "S")
-        back_add(2, (0,))
-        back_turn(2, (2,))
-        back_add(2, (1,))
-        back_turn(2, (3,))
-        turn("h6", (1,))
-        lay("h6", 1, "S")
-        back_add(2, (2, 3,))
-        store(2)
-        lay("x5", 1, "V")
-        gate[4] = work.tile([P, NT * RG], F32, name="gate4", tag="gate", bufs=GATE_BUFS)
-        mx_pass("wu", "x4", (0, 1, 2, 3,))
-        qz("x5")
-        qz("h6")
-        load_rows("h", 8)
-        load_rows("x", 7)
-        mx_act("x4", gate[4], ACT.Sigmoid, 0, (0, 1, 2, 3,))
-        mul_gate(4, "G", 0, 1024)
-        mul_gate(4, "G", 1024, 2048)
-        back_turn(3, (0, 1,))
-        cand[6] = work.tile([P, NT * RG], F32, name="cand6", tag="cand", bufs=CAND_BUFS)
-        mx_pass("wh", "h6", (0, 1, 2, 3,))
-        mx_act("h6", cand[6], ACT.Tanh, 4, (0, 1, 2, 3,))
-        turn("h7", (0,))
-        sub_x(5, 0)
-        turn("x6", (0,))
-        sub_x(5, 1)
-        turn("x6", (1,))
-        lay("h7", 0, "S")
-        lay("x6", 0, "S")
-        back_add(3, (0,))
-        back_turn(3, (2,))
-        back_add(3, (1,))
-        back_turn(3, (3,))
-        turn("h7", (1,))
-        lay("h7", 1, "S")
-        back_add(3, (2, 3,))
-        store(3)
-        lay("x6", 1, "V")
-        gate[5] = work.tile([P, NT * RG], F32, name="gate5", tag="gate", bufs=GATE_BUFS)
-        mx_pass("wu", "x5", (0, 1, 2, 3,))
-        qz("x6")
-        qz("h7")
-        load_rows("h", 9)
-        load_rows("x", 8)
-        mx_act("x5", gate[5], ACT.Sigmoid, 0, (0, 1, 2, 3,))
-        mul_gate(5, "G", 0, 1024)
-        mul_gate(5, "G", 1024, 2048)
-        back_turn(4, (0, 1,))
-        cand[7] = work.tile([P, NT * RG], F32, name="cand7", tag="cand", bufs=CAND_BUFS)
-        mx_pass("wh", "h7", (0, 1, 2, 3,))
-        mx_act("h7", cand[7], ACT.Tanh, 4, (0, 1, 2, 3,))
-        turn("h8", (0,))
-        sub_x(6, 0)
-        turn("x7", (0,))
-        sub_x(6, 1)
-        turn("x7", (1,))
-        lay("h8", 0, "S")
-        lay("x7", 0, "S")
-        back_add(4, (0,))
-        back_turn(4, (2,))
-        back_add(4, (1,))
-        back_turn(4, (3,))
-        turn("h8", (1,))
-        lay("h8", 1, "S")
-        back_add(4, (2, 3,))
-        store(4)
-        lay("x7", 1, "V")
-        gate[6] = work.tile([P, NT * RG], F32, name="gate6", tag="gate", bufs=GATE_BUFS)
-        mx_pass("wu", "x6", (0, 1, 2, 3,))
-        qz("x7")
-        qz("h8")
-        load_rows("h", 10)
-        load_rows("x", 9)
-        mx_act("x6", gate[6], ACT.Sigmoid, 0, (0, 1, 2, 3,))
-        mul_gate(6, "G", 0, 1024)
-        mul_gate(6, "G", 1024, 2048)
-        back_turn(5, (0, 1,))
-        cand[8] = work.tile([P, NT * RG], F32, name="cand8", tag="cand", bufs=CAND_BUFS)
-        mx_pass("wh", "h8", (0, 1, 2, 3,))
-        mx_act("h8", cand[8], ACT.Tanh, 4, (0, 1, 2, 3,))
-        turn("h9", (0,))
-        sub_x(7, 0)
-        turn("x8", (0,))
-        sub_x(7, 1)
-        turn("x8", (1,))
-        lay("h9", 0, "S")
-        lay("x8", 0, "S")
-        back_add(5, (0,))
-        back_turn(5, (2,))
-        back_add(5, (1,))
-        back_turn(5, (3,))
-        turn("h9", (1,))
-        lay("h9", 1, "S")
-        back_add(5, (2, 3,))
-        store(5)
-        lay("x8", 1, "V")
-        gate[7] = work.tile([P, NT * RG], F32, name="gate7", tag="gate", bufs=GATE_BUFS)
-        mx_pass("wu", "x7", (0, 1, 2, 3,))
-        qz("x8")
-        qz("h9")
-        load_rows("h", 11)
-        load_rows("x", 10)
-        mx_act("x7", gate[7], ACT.Sigmoid, 0, (0, 1, 2, 3,))
-        mul_gate(7, "G", 0, 1024)
-        mul_gate(7, "G", 1024, 2048)
-        back_turn(6, (0, 1,))
-        cand[9] = work.tile([P, NT * RG], F32, name="cand9", tag="cand", bufs=CAND_BUFS)
-        mx_pass("wh", "h9", (0, 1, 2, 3,))
-        mx_act("h9", cand[9], ACT.Tanh, 4, (0, 1, 2, 3,))
-        turn("h10", (0,))
-        sub_x(8, 0)
-        turn("x9", (0,))
-        sub_x(8, 1)
-        turn("x9", (1,))
-        lay("h10", 0, "S")
-        lay("x9", 0, "S")
-        back_add(6, (0,))
-        back_turn(6, (2,))
-        back_add(6, (1,))
-        back_turn(6, (3,))
-        turn("h10", (1,))
-        lay("h10", 1, "S")
-        back_add(6, (2, 3,))
-        store(6)
-        lay("x9", 1, "V")
-        gate[8] = work.tile([P, NT * RG], F32, name="gate8", tag="gate", bufs=GATE_BUFS)
-        mx_pass("wu", "x8", (0, 1, 2, 3,))
-        qz("x9")
-        qz("h10")
-        load_rows("h", 12)
-        load_rows("x", 11)
-        mx_act("x8", gate[8], ACT.Sigmoid, 0, (0, 1, 2, 3,))
-        mul_gate(8, "G", 0, 1024)
-        mul_gate(8, "G", 1024, 2048)
-        back_turn(7, (0, 1,))
-        cand[10] = work.tile([P, NT * RG], F32, name="cand10", tag="cand", bufs=CAND_BUFS)
-        mx_pass("wh", "h10", (0, 1, 2, 3,))
-        mx_act("h10", cand[10], ACT.Tanh, 4, (0, 1, 2, 3,))
-        turn("h11", (0,))
-        sub_x(9, 0)
-        turn("x10", (0,))
-        sub_x(9, 1)
-        turn("x10", (1,))
-        lay("h11", 0, "S")
-        lay("x10", 0, "S")
-        back_add(7, (0,))
-        back_turn(7, (2,))
-        back_add(7, (1,))
-        back_turn(7, (3,))
-        turn("h11", (1,))
-        lay("h11", 1, "S")
-        back_add(7, (2, 3,))
-        store(7)
-        lay("x10", 1, "V")
-        gate[9] = work.tile([P, NT * RG], F32, name="gate9", tag="gate", bufs=GATE_BUFS)
-        mx_pass("wu", "x9", (0, 1, 2, 3,))
-        qz("x10")
-        qz("h11")
-        load_rows("h", 13)
-        load_rows("x", 12)
-        mx_act("x9", gate[9], ACT.Sigmoid, 0, (0, 1, 2, 3,))
-        mul_gate(9, "G", 0, 1024)
-        mul_gate(9, "G", 1024, 2048)
-        back_turn(8, (0, 1,))
-        cand[11] = work.tile([P, NT * RG], F32, name="cand11", tag="cand", bufs=CAND_BUFS)
-        mx_pass("wh", "h11", (0, 1, 2, 3,))
-        mx_act("h11", cand[11], ACT.Tanh, 4, (0, 1, 2, 3,))
-        turn("h12", (0,))
-        sub_x(10, 0)
-        turn("x11", (0,))
-        sub_x(10, 1)
-        turn("x11", (1,))
-        lay("h12", 0, "S")
-        lay("x11", 0, "S")
-        back_add(8, (0,))
-        back_turn(8, (2,))
-        back_add(8, (1,))
-        back_turn(8, (3,))
-        turn("h12", (1,))
-        lay("h12", 1, "S")
-        back_add(8, (2, 3,))
-        store(8)
-        lay("x11", 1, "V")
-        gate[10] = work.tile([P, NT * RG], F32, name="gate10", tag="gate", bufs=GATE_BUFS)
-        mx_pass("wu", "x10", (0, 1, 2, 3,))
-        qz("x11")
-        qz("h12")
-        load_rows("h", 14)
-        load_rows("x", 13)
-        mx_act("x10", gate[10], ACT.Sigmoid, 0, (0, 1, 2, 3,))
-        mul_gate(10, "G", 0, 1024)
-        mul_gate(10, "G", 1024, 2048)
-        back_turn(9, (0, 1,))
-        cand[12] = work.tile([P, NT * RG], F32, name="cand12", tag="cand", bufs=CAND_BUFS)
-        mx_pass("wh", "h12", (0, 1, 2, 3,))
-        mx_act("h12", cand[12], ACT.Tanh, 4, (0, 1, 2, 3,))
-        turn("h13", (0,))
-        sub_x(11, 0)
-        turn("x12", (0,))
-        sub_x(11, 1)
-        turn("x12", (1,))
-        lay("h13", 0, "S")
-        lay("x12", 0, "S")
-        back_add(9, (0,))
-        back_turn(9, (2,))
-        back_add(9, (1,))
-        back_turn(9, (3,))
-        turn("h13", (1,))
-        lay("h13", 1, "S")
-        back_add(9, (2, 3,))
-        store(9)
-        lay("x12", 1, "V")
-        gate[11] = work.tile([P, NT * RG], F32, name="gate11", tag="gate", bufs=GATE_BUFS)
-        mx_pass("wu", "x11", (0, 1, 2, 3,))
-        qz("x12")
-        qz("h13")
-        load_rows("h", 15)
-        load_rows("x", 14)
-        mx_act("x11", gate[11], ACT.Sigmoid, 0, (0, 1, 2, 3,))
-        mul_gate(11, "G", 0, 1024)
-        mul_gate(11, "G", 1024, 2048)
-        back_turn(10, (0, 1,))
-        cand[13] = work.tile([P, NT * RG], F32, name="cand13", tag="cand", bufs=CAND_BUFS)
-        mx_pass("wh", "h13", (0, 1, 2, 3,))
-        mx_act("h13", cand[13], ACT.Tanh, 4, (0, 1, 2, 3,))
-        turn("h14", (0,))
-        sub_x(12, 0)
-        turn("x13", (0,))
-        sub_x(12, 1)
-        turn("x13", (1,))
-        lay("h14", 0, "S")
-        lay("x13", 0, "S")
-        back_add(10, (0,))
-        back_turn(10, (2,))
-        back_add(10, (1,))
-        back_turn(10, (3,))
-        turn("h14", (1,))
-        lay("h14", 1, "S")
-        back_add(10, (2, 3,))
-        store(10)
-        lay("x13", 1, "V")
-        gate[12] = work.tile([P, NT * RG], F32, name="gate12", tag="gate", bufs=GATE_BUFS)
-        mx_pass("wu", "x12", (0, 1, 2, 3,))
-        qz("x13")
-        qz("h14")
-        load_rows("x", 15)
-        mx_act("x12", gate[12], ACT.Sigmoid, 0, (0, 1, 2, 3,))
-        mul_gate(12, "G", 0, 1024)
-        mul_gate(12, "G", 1024, 2048)
-        back_turn(11, (0, 1,))
-        cand[14] = work.tile([P, NT * RG], F32, name="cand14", tag="cand", bufs=CAND_BUFS)
-        mx_pass("wh", "h14", (0, 1, 2, 3,))
-        mx_act("h14", cand[14], ACT.Tanh, 4, (0, 1, 2, 3,))
-        turn("h15", (0,))
-        sub_x(13, 0)
-        turn("x14", (0,))
-        sub_x(13, 1)
-        turn("x14", (1,))
-        lay("h15", 0, "S")
-        lay("x14", 0, "S")
-        back_add(11, (0,))
-        back_turn(11, (2,))
-        back_add(11, (1,))
-        back_turn(11, (3,))
-        turn("h15", (1,))
-        lay("h15", 1, "S")
-        back_add(11, (2, 3,))
-        store(11)
-        lay("x14", 1, "V")
-        gate[13] = work.tile([P, NT * RG], F32, name="gate13", tag="gate", bufs=GATE_BUFS)
-        mx_pass("wu", "x13", (0, 1, 2, 3,))
-        qz("x14")
-        qz("h15")
-        mx_act("x13", gate[13], ACT.Sigmoid, 0, (0, 1, 2, 3,))
-        sub_x(14, 0)
-        back_turn(12, (0, 1,))
-        sub_x(14, 1)
-        mul_gate(13, "G", 0, 1024)
-        cand[15] = work.tile([P, NT * RG], F32, name="cand15", tag="cand", bufs=CAND_BUFS)
-        mx_pass("wh", "h15", (0, 1, 2, 3,))
-        turn("x15", (0,))
-        mx_act("h15", cand[15], ACT.Tanh, 4, (0, 1, 2, 3,))
-        turn("x15", (1,))
-        back_turn(12, (2,))
-        gate[14] = work.tile([P, NT * RG], F32, name="gate14", tag="gate", bufs=GATE_BUFS)
-        mx_pass("wu", "x14", (0, 1, 2, 3,))
-        mul_gate(13, "G", 1024, 2048)
-        lay("x15", 0, "S")
-        mx_act("x14", gate[14], ACT.Sigmoid, 0, (0, 1, 2, 3,))
-        back_add(12, (0,))
-        back_turn(12, (3,))
-        back_add(12, (1,))
-        lay("x15", 1, "V")
-        qz("x15")
-        back_add(12, (2, 3,))
-        sub_x(15, 1)
-        mul_gate(14, "G", 0, 1024)
-        back_turn(13, (0, 1,))
-        back_add(13, (0,))
-        store(12)
-        sub_x(15, 0)
-        gate[15] = work.tile([P, NT * RG], F32, name="gate15", tag="gate", bufs=GATE_BUFS)
-        mx_pass("wu", "x15", (0, 1, 2, 3,))
-        back_turn(13, (2,))
-        back_turn(13, (3,))
-        back_add(13, (1,))
-        mul_gate(14, "G", 1024, 2048)
-        back_turn(14, (0, 1,))
-        back_add(13, (2, 3,))
-        mx_act("x15", gate[15], ACT.Sigmoid, 0, (0, 1, 2, 3,))
-        back_add(14, (0,))
-        mul_gate(15, "G", 0, 1024)
-        back_turn(14, (2,))
-        back_turn(14, (3,))
-        back_add(14, (1,))
-        store(13)
-        mul_gate(15, "G", 1024, 2048)
-        back_add(14, (2, 3,))
-        back_turn(15, (0, 1,))
-        back_turn(15, (2,))
-        back_turn(15, (3,))
-        store(14)
-        back_add(15, (0,))
-        back_add(15, (1,))
-        back_add(15, (2, 3,))
+
+        bias_bank = psum.tile([P, GROUP], F32, name="T_bias", tag="hT", bufs=BANKS["hT"])
+        nc.tensor.transpose(bias_bank[:, 0:P], bias_rows[:].bitcast(F32), identity[:])
+        nc.vector.tensor_copy(out=bias[:], in_=bias_bank[:, 0:TILES].bitcast(BF16))
+
+        for name, g, role, copy in (
+            ("Wh", 0, "xT", scalar_copy),
+            ("h", 0, "back", scalar_copy),
+            ("Wu", 0, "xT", scalar_copy),
+            ("h", 1, "back", vector_copy),
+        ):
+            turn(name, g, (0, 1), role)
+            lay(name, g, 0, copy)
+            lay(name, g, 1, copy)
+            if name != "Wu":
+                quantise(name, g)
+        passes("h", 0)
+        activate("h", 0)
+        quantise("Wu", 0)
+        turn("x", 0, (0, 1), "xT")
+        lay("x", 0, 0, vector_copy)
+        lay("x", 0, 1, vector_copy)
+        quantise("x", 0)
+        passes("h", 1)
+        activate("h", 1)
+        turn("h", 2, (0,), "hT")
+        turn("x", 1, (0, 1), "back")
+        turn("h", 2, (1,), "hT")
+        subtract_query(0, 0)
+        lay("x", 1, 0, vector_copy)
+        subtract_query(0, 1)
+        passes("x", 0)
+        lay("h", 2, 0, scalar_copy)
+        lay("x", 1, 1, scalar_copy)
+        lay("h", 2, 1, scalar_copy)
+
+        for i in range(GROUPS + 1):
+            load_rows("h", i + 4)
+            load_rows("x", i + 3)
+            quantise("x", i + 1)
+            quantise("h", i + 2)
+            activate("x", i)
+            if not live(i + 2):
+                passes("x", i + 1)
+            multiply_gate(i)
+            turn_back(i - 1, (0, 1))
+            passes("h", i + 2)
+            activate("h", i + 2)
+            turn("h", i + 3, (0,), "hT")
+            subtract_query(i + 1, 0)
+            turn("x", i + 2, (0,), "xT")
+            subtract_query(i + 1, 1)
+            turn("x", i + 2, (1,), "xT")
+            lay("h", i + 3, 0, scalar_copy)
+            lay("x", i + 2, 0, scalar_copy)
+            add_query(i - 1, 0)
+            turn_back(i - 1, (2,))
+            add_query(i - 1, 1)
+            turn_back(i - 1, (3,))
+            turn("h", i + 3, (1,), "hT")
+            lay("h", i + 3, 1, scalar_copy)
+            lay("x", i + 2, 1, vector_copy)
+            add_query(i - 1, 2)
+            add_query(i - 1, 3)
+            store(i - 1)
+            if live(i + 2):
+                passes("x", i + 1)

@@ -22,7 +22,7 @@ FLOPS = 2 * 2 * ROWS * E * E
 
 BANKS = {"xT": 2, "hT": 1, "mx": 3, "back": 2}
 WEIGHTS = {"h": "Wh", "x": "Wu"}
-ROW_SLOTS = {"h": 4, "x": 6}
+ROW_SLOTS = {"h": 5, "x": 6}
 RESULT_SLOTS = {"h": 5, "x": 2}
 OUT_SLOTS = 3
 STREAM_SLOTS = 2
@@ -108,14 +108,15 @@ def tile_gatedcrossattention_pb_t_kernel(tc, query, hr, Wu, bu, Wh, bh, out):
                 codes[(name, g)] = words
                 scales[(name, g)] = plane
 
-        def passes(name, g):
+        def passes(name, g, feature_tiles):
             if not live(g):
                 return
             w = (WEIGHTS[name], 0)
-            result[(name, g)] = work.tile(
-                [P, TILES * GROUP], F32, name="result_%s%d" % (name, g), tag="result_" + name, bufs=RESULT_SLOTS[name]
-            )
-            for t in range(TILES):
+            if feature_tiles[0] == 0:
+                result[(name, g)] = work.tile(
+                    [P, TILES * GROUP], F32, name="result_%s%d" % (name, g), tag="result_" + name, bufs=RESULT_SLOTS[name]
+                )
+            for t in feature_tiles:
                 bank = psum.tile([P, GROUP], F32, name="mx_%s%d_%d" % (name, g, t), tag="mx", bufs=BANKS["mx"])
                 nc.tensor.matmul_mx(
                     out=bank[:],
@@ -128,10 +129,10 @@ def tile_gatedcrossattention_pb_t_kernel(tc, query, hr, Wu, bu, Wh, bh, out):
                 )
                 sums[(name, g, t)] = bank
 
-        def activate(name, g):
+        def activate(name, g, feature_tiles):
             if live(g):
                 func, column = (ACT.Tanh, TILES) if name == "h" else (ACT.Sigmoid, 0)
-                for t in range(TILES):
+                for t in feature_tiles:
                     nc.scalar.activation(
                         out=result[(name, g)][:, t * GROUP:(t + 1) * GROUP], in_=sums[(name, g, t)][:], func=func,
                         bias=bias[:, column + t:column + t + 1], scale=1.0,
@@ -210,6 +211,7 @@ def tile_gatedcrossattention_pb_t_kernel(tc, query, hr, Wu, bu, Wh, bh, out):
         load_rows("h", 2)
         load_rows("h", 3)
         load_rows("x", 2)
+        load_rows("h", 4)
 
         bias_bank = psum.tile([P, GROUP], F32, name="T_bias", tag="hT", bufs=BANKS["hT"])
         nc.tensor.transpose(bias_bank[:, 0:P], bias_rows[:].bitcast(F32), identity[:])
@@ -226,54 +228,57 @@ def tile_gatedcrossattention_pb_t_kernel(tc, query, hr, Wu, bu, Wh, bh, out):
             lay(name, g, 1, copy)
             if name != "Wu":
                 quantise(name, g)
-        passes("h", 0)
-        activate("h", 0)
+        passes("h", 0, (0, 1, 2, 3))
+        activate("h", 0, (0, 1, 2, 3))
         quantise("Wu", 0)
         turn("x", 0, (0, 1), "xT")
         lay("x", 0, 0, vector_copy)
         lay("x", 0, 1, vector_copy)
         quantise("x", 0)
-        passes("h", 1)
-        activate("h", 1)
+        passes("h", 1, (0, 1, 2, 3))
+        activate("h", 1, (0, 1, 2, 3))
         turn("h", 2, (0,), "hT")
         turn("x", 1, (0, 1), "back")
         turn("h", 2, (1,), "hT")
         subtract_query(0, 0)
         lay("x", 1, 0, vector_copy)
         subtract_query(0, 1)
-        passes("x", 0)
+        passes("x", 0, (0, 1, 2))
         lay("h", 2, 0, scalar_copy)
         lay("x", 1, 1, scalar_copy)
         lay("h", 2, 1, scalar_copy)
+        turn("h", 3, (0,), "hT")
+        lay("h", 3, 0, scalar_copy)
 
         for i in range(GROUPS + 1):
-            load_rows("h", i + 4)
+            load_rows("h", i + 5)
             load_rows("x", i + 3)
-            quantise("x", i + 1)
             quantise("h", i + 2)
-            activate("x", i)
-            if not live(i + 2):
-                passes("x", i + 1)
-            multiply_gate(i)
+            quantise("x", i + 1)
+            activate("x", i, (0, 1, 2))
             turn_back(i - 1, (0, 1))
-            passes("h", i + 2)
-            activate("h", i + 2)
-            turn("h", i + 3, (0,), "hT")
+            turn("h", i + 3, (1,), "hT")
+            lay("h", i + 3, 1, scalar_copy)
+            passes("x", i, (3,))
+            activate("x", i, (3,))
+            multiply_gate(i)
+            passes("h", i + 2, (0, 1))
+            activate("h", i + 2, (0, 1))
             subtract_query(i + 1, 0)
             turn("x", i + 2, (0,), "xT")
+            turn("h", i + 4, (0,), "hT")
+            passes("h", i + 2, (2, 3))
+            activate("h", i + 2, (2, 3))
             subtract_query(i + 1, 1)
             turn("x", i + 2, (1,), "xT")
-            lay("h", i + 3, 0, scalar_copy)
-            lay("x", i + 2, 0, scalar_copy)
             add_query(i - 1, 0)
             turn_back(i - 1, (2,))
             add_query(i - 1, 1)
             turn_back(i - 1, (3,))
-            turn("h", i + 3, (1,), "hT")
-            lay("h", i + 3, 1, scalar_copy)
+            lay("x", i + 2, 0, scalar_copy)
+            lay("h", i + 4, 0, scalar_copy)
             lay("x", i + 2, 1, vector_copy)
             add_query(i - 1, 2)
             add_query(i - 1, 3)
             store(i - 1)
-            if live(i + 2):
-                passes("x", i + 1)
+            passes("x", i + 1, (0, 1, 2))

@@ -145,22 +145,21 @@ def tile_gatedcrossattention_pb_t_kernel(tc, query, hr, Wu, bu, Wh, bh, out):
                 nc.vector.tensor_tensor(out=c, in0=c, in1=x_t, op=ALU.subtract)
 
         def multiply_gate(g):
-            if not live(g):
-                return
-            d = result[("h", g)][:].rearrange("p (t r) -> p t r", t=TILES)
-            u = result[("x", g)][:].rearrange("p (t r) -> p t r", t=TILES)
-            if g < GROUPS - 1:
+            if live(g):
                 for t in (0, 2):
-                    nc.gpsimd.tensor_tensor(out=d[:, t:t + 2, :], in0=u[:, t:t + 2, :], in1=d[:, t:t + 2, :], op=ALU.mult)
-            else:
-                for j in range(TILES):
-                    cut = slice(j * P, (j + 1) * P)
-                    nc.gpsimd.tensor_tensor(out=d[:, :, cut], in0=u[:, :, cut], in1=d[:, :, cut], op=ALU.mult)
+                    half = slice(t * GROUP, (t + 2) * GROUP)
+                    d = result[("h", g)][:, half]
+                    nc.gpsimd.tensor_tensor(out=d, in0=result[("x", g)][:, half], in1=d, op=ALU.mult)
 
-        def turn_back(g, row_tiles):
+        def multiply_row_tile(g, j, engine):
+            d = result[("h", g)][:].rearrange("p (t r) -> p t r", t=TILES)[:, :, j * P:(j + 1) * P]
+            u = result[("x", g)][:].rearrange("p (t r) -> p t r", t=TILES)[:, :, j * P:(j + 1) * P]
+            engine.tensor_tensor(out=d, in0=u, in1=d, op=ALU.mult)
+
+        def turn_back(g, row_tiles, role="back"):
             if live(g):
                 for j in row_tiles:
-                    bank = psum.tile([P, E], F32, name="back_%d_%d" % (g, j), tag="back", bufs=BANKS["back"])
+                    bank = psum.tile([P, E], F32, name="back_%d_%d" % (g, j), tag=role, bufs=BANKS[role])
                     for t in range(TILES):
                         nc.tensor.transpose(
                             bank[:, t * P:(t + 1) * P], result[("h", g)][:, t * GROUP + j * P:t * GROUP + (j + 1) * P], identity[:]
@@ -170,7 +169,7 @@ def tile_gatedcrossattention_pb_t_kernel(tc, query, hr, Wu, bu, Wh, bh, out):
         def add_query(g, j):
             if not live(g):
                 return
-            if j == 0:
+            if g not in blended:
                 blended[g] = rows.tile([P, TILES * E], F32, name="out_%d" % g, tag="out", bufs=OUT_SLOTS)
             cut = slice(j * E, (j + 1) * E)
             nc.vector.tensor_tensor(
@@ -237,25 +236,30 @@ def tile_gatedcrossattention_pb_t_kernel(tc, query, hr, Wu, bu, Wh, bh, out):
         quantise("x", 0)
         passes("h", 1, (0, 1, 2, 3))
         activate("h", 1, (0, 1, 2, 3))
-        turn("h", 2, (0,), "hT")
-        turn("x", 1, (0, 1), "back")
-        turn("h", 2, (1,), "hT")
+        turn("h", 2, (0, 1), "back")
         subtract_query(0, 0)
-        lay("x", 1, 0, vector_copy)
-        subtract_query(0, 1)
         passes("x", 0, (0, 1, 2))
-        lay("h", 2, 0, scalar_copy)
-        lay("x", 1, 1, scalar_copy)
-        lay("h", 2, 1, scalar_copy)
-        turn("h", 3, (0,), "hT")
-        lay("h", 3, 0, scalar_copy)
+        lay("h", 2, 0, vector_copy)
+        lay("h", 2, 1, vector_copy)
+        quantise("h", 2)
+        turn("x", 1, (0,), "xT")
+        activate("x", 0, (0,))
+        lay("x", 1, 0, scalar_copy)
+        turn("h", 3, (0,), "back")
+        subtract_query(0, 1)
+        turn("x", 1, (1,), "xT")
+        lay("x", 1, 1, vector_copy)
 
-        for i in range(GROUPS + 1):
+        for i in range(GROUPS - 2):
             load_rows("h", i + 5)
             load_rows("x", i + 3)
-            quantise("h", i + 2)
-            quantise("x", i + 1)
-            activate("x", i, (0, 1, 2))
+            if i > 0:
+                quantise("h", i + 2)
+                quantise("x", i + 1)
+                activate("x", i, (0,))
+            activate("x", i, (1, 2))
+            if i == 0:
+                lay("h", 3, 0, scalar_copy)
             turn_back(i - 1, (0, 1))
             turn("h", i + 3, (1,), "hT")
             lay("h", i + 3, 1, scalar_copy)
@@ -265,6 +269,8 @@ def tile_gatedcrossattention_pb_t_kernel(tc, query, hr, Wu, bu, Wh, bh, out):
             passes("h", i + 2, (0, 1))
             activate("h", i + 2, (0, 1))
             subtract_query(i + 1, 0)
+            if i == 0:
+                quantise("x", 1)
             turn("x", i + 2, (0,), "xT")
             turn("h", i + 4, (0,), "hT")
             passes("h", i + 2, (2, 3))
@@ -282,3 +288,38 @@ def tile_gatedcrossattention_pb_t_kernel(tc, query, hr, Wu, bu, Wh, bh, out):
             add_query(i - 1, 3)
             store(i - 1)
             passes("x", i + 1, (0, 1, 2))
+
+        last = GROUPS - 1
+        quantise("x", last)
+        activate("x", last - 1, (0, 1, 2))
+        turn_back(last - 2, (0, 1))
+        turn_back(last - 2, (2,), "hT")
+        passes("x", last - 1, (3,))
+        activate("x", last - 1, (3,))
+        multiply_gate(last - 1)
+        passes("x", last, (0, 1, 2))
+        activate("x", last, (0, 1, 2))
+        subtract_query(last, 0)
+        add_query(last - 2, 0)
+        turn_back(last - 2, (3,))
+        passes("x", last, (3,))
+        activate("x", last, (3,))
+        subtract_query(last, 1)
+        add_query(last - 2, 1)
+        add_query(last - 2, 2)
+        add_query(last - 2, 3)
+        store(last - 2)
+        turn_back(last - 1, (0, 1), "xT")
+        turn_back(last - 1, (2, 3))
+        multiply_row_tile(last, 3, nc.vector)
+        for j in range(3):
+            multiply_row_tile(last, j, nc.gpsimd)
+        turn_back(last, (3,), "hT")
+        for j in range(TILES):
+            add_query(last - 1, j)
+        store(last - 1)
+        turn_back(last, (0, 1), "xT")
+        turn_back(last, (2,))
+        add_query(last, 3)
+        for j in range(3):
+            add_query(last, j)

@@ -25,7 +25,7 @@ WEIGHTS = {"h": "Wh", "x": "Wu"}
 ROW_SLOTS = {"h": 5, "x": 6}
 RESULT_SLOTS = {"h": 5, "x": 2}
 OUT_SLOTS = 3
-STREAM_SLOTS = 2
+PAIR_SLOTS = {"grouped": 3, "codes": 2, "scales": 2}
 
 
 def tile_gatedcrossattention_pb_t_kernel(tc, query, hr, Wu, bu, Wh, bh, out):
@@ -52,9 +52,6 @@ def tile_gatedcrossattention_pb_t_kernel(tc, query, hr, Wu, bu, Wh, bh, out):
 
         def live(g):
             return 0 <= g < GROUPS
-
-        def slots(name):
-            return STREAM_SLOTS if name in WEIGHTS else 1
 
         def group_view(flat, g):
             return flat[g * GROUP:(g + 1) * GROUP, :].rearrange("(p j) e -> p j e", j=TILES)
@@ -90,40 +87,52 @@ def tile_gatedcrossattention_pb_t_kernel(tc, query, hr, Wu, bu, Wh, bh, out):
                         )
                 banks[(name, g, half)] = bank
 
+        def operand(tiles, name, g, width, dtype, what):
+            key = (name, g) if name in WEIGHTS.values() else g - 2 if name == "h" else g - 1
+            if key not in tiles:
+                label = name if name in WEIGHTS.values() else "pair%d" % (key + 2)
+                tiles[key] = work.tile(
+                    [P, width if name in WEIGHTS.values() else 2 * width], dtype, name=what + "_" + label,
+                    tag=what + ("_" + name if name in WEIGHTS.values() else ""), bufs=1 if name in WEIGHTS.values() else PAIR_SLOTS[what], align_bytes=64,
+                )
+            return tiles[key], width if name == "x" else 0
+
         def lay(name, g, half, engine):
             if not live(g):
                 return
-            if half == 0:
-                grouped[(name, g)] = work.tile(
-                    [P, TILES * GROUP], BF16, name="grouped_%s%d" % (name, g), tag="grouped_" + name, bufs=slots(name), align_bytes=64
-                )
-            dst = grouped[(name, g)][:].bitcast(F32)[:, half * GROUP:(half + 1) * GROUP]
+            tile_, first = operand(grouped, name, g, TILES * GROUP, BF16, "grouped")
+            dst = tile_[:].bitcast(F32)[:, first // 2 + half * GROUP:first // 2 + (half + 1) * GROUP]
             engine(out=dst.rearrange("p (r a) -> p r a", a=2), in_=banks[(name, g, half)][:].rearrange("p (a r) -> p r a", a=2))
 
-        def quantise(name, g):
+        def quantise(name, g, both=False):
             if live(g):
-                words = work.tile([P, GROUP], U32, name="codes_%s%d" % (name, g), tag="codes_" + name, bufs=slots(name), align_bytes=64)
-                plane = work.tile([P, GROUP], U8, name="scales_%s%d" % (name, g), tag="scales_" + name, bufs=slots(name), align_bytes=64)
-                nc.vector.quantize_mx(out=words[:].bitcast(FP8X4), scales=plane[:], in_=grouped[(name, g)][:])
-                codes[(name, g)] = words
-                scales[(name, g)] = plane
+                src, first = operand(grouped, name, g, TILES * GROUP, BF16, "grouped")
+                words, at = operand(codes, name, g, GROUP, U32, "codes")
+                plane, at = operand(scales, name, g, GROUP, U8, "scales")
+                count = 2 if both else 1
+                nc.vector.quantize_mx(
+                    out=words[:, at:at + count * GROUP].bitcast(FP8X4), scales=plane[:, at:at + count * GROUP],
+                    in_=src[:, first:first + count * TILES * GROUP],
+                )
 
         def passes(name, g, feature_tiles):
             if not live(g):
                 return
-            w = (WEIGHTS[name], 0)
             if feature_tiles[0] == 0:
                 result[(name, g)] = work.tile(
                     [P, TILES * GROUP], F32, name="result_%s%d" % (name, g), tag="result_" + name, bufs=RESULT_SLOTS[name]
                 )
             for t in feature_tiles:
                 bank = psum.tile([P, GROUP], F32, name="mx_%s%d_%d" % (name, g, t), tag="mx", bufs=BANKS["mx"])
+                codes_w, scales_w = codes[(WEIGHTS[name], 0)], scales[(WEIGHTS[name], 0)]
+                words, at = operand(codes, name, g, GROUP, U32, "codes")
+                plane, at = operand(scales, name, g, GROUP, U8, "scales")
                 nc.tensor.matmul_mx(
                     out=bank[:],
-                    lhsT=codes[w][:, t * P:(t + 1) * P].bitcast(FP8X4),
-                    lhsT_scale=scales[w][:, t * P:(t + 1) * P],
-                    rhs=codes[(name, g)][:].bitcast(FP8X4),
-                    rhs_scale=scales[(name, g)][:],
+                    lhsT=codes_w[:, t * P:(t + 1) * P].bitcast(FP8X4),
+                    lhsT_scale=scales_w[:, t * P:(t + 1) * P],
+                    rhs=words[:, at:at + GROUP].bitcast(FP8X4),
+                    rhs_scale=plane[:, at:at + GROUP],
                     start=True,
                     stop=True,
                 )
@@ -166,6 +175,31 @@ def tile_gatedcrossattention_pb_t_kernel(tc, query, hr, Wu, bu, Wh, bh, out):
                         )
                     turned[(g, j)] = bank
 
+        def place_query(g, j, role):
+            bank = psum.tile([P, E], F32, name="back_%d_%d" % (g, j), tag=role, bufs=BANKS[role])
+            nc.tensor.matmul(
+                bank[:].rearrange("p (a e m) -> p a e m", a=2, e=2), lhsT=identity_bf16[:],
+                rhs=loaded[("x", g)][:, j * E:(j + 1) * E].rearrange("p (a m e) -> p a e m", a=2, e=2), start=True, stop=False,
+            )
+            turned[(g, j)] = bank
+
+        def turn_back_onto_query(g, j):
+            for t in range(TILES):
+                nc.tensor.matmul(
+                    turned[(g, j)][:, t * P:(t + 1) * P], lhsT=result[("h", g)][:, t * GROUP + j * P:t * GROUP + (j + 1) * P], rhs=identity[:],
+                    is_transpose=True, start=False, stop=t == TILES - 1,
+                )
+
+        def copy_back(g, j, engine):
+            if g not in blended:
+                blended[g] = rows.tile([P, TILES * E], F32, name="out_%d" % g, tag="out", bufs=OUT_SLOTS)
+            cut = slice(j * E, (j + 1) * E)
+            engine(
+                out=blended[g][:, cut].rearrange("p (a m e) -> p a m e", a=2, e=2),
+                in_=turned[(g, j)][:].rearrange("p (a e m) -> p a m e", a=2, e=2),
+            )
+            nc.sync.dma_start(out=group_view(out_rows, g)[:, j, :], in_=blended[g][:, cut])
+
         def add_query(g, j):
             if not live(g):
                 return
@@ -196,6 +230,8 @@ def tile_gatedcrossattention_pb_t_kernel(tc, query, hr, Wu, bu, Wh, bh, out):
         nc.scalar.activation(out=warm[:], in_=zero[:], func=ACT.Sigmoid)
         identity = const.tile([P, P], F32, name="identity")
         make_identity(nc, identity[:])
+        identity_bf16 = const.tile([P, P], BF16, name="identity_bf16")
+        nc.gpsimd.tensor_copy(out=identity_bf16[:], in_=identity[:])
         bias = const.tile([P, 2 * TILES], F32, name="bias")
 
         scalar_copy = nc.scalar.copy
@@ -216,15 +252,15 @@ def tile_gatedcrossattention_pb_t_kernel(tc, query, hr, Wu, bu, Wh, bh, out):
         nc.tensor.transpose(bias_bank[:, 0:P], bias_rows[:].bitcast(F32), identity[:])
         nc.vector.tensor_copy(out=bias[:], in_=bias_bank[:, 0:TILES].bitcast(BF16))
 
-        for name, g, role, copy in (
-            ("Wh", 0, "xT", scalar_copy),
-            ("h", 0, "back", scalar_copy),
-            ("Wu", 0, "xT", scalar_copy),
-            ("h", 1, "back", vector_copy),
+        for name, g, role, engines in (
+            ("Wh", 0, "xT", (scalar_copy, scalar_copy)),
+            ("h", 0, "back", (scalar_copy, scalar_copy)),
+            ("Wu", 0, "xT", (scalar_copy, scalar_copy)),
+            ("h", 1, "back", (scalar_copy, vector_copy)),
         ):
             turn(name, g, (0, 1), role)
-            lay(name, g, 0, copy)
-            lay(name, g, 1, copy)
+            for half in range(2):
+                lay(name, g, half, engines[half])
             if name != "Wu":
                 quantise(name, g)
         passes("h", 0, (0, 1, 2, 3))
@@ -236,32 +272,33 @@ def tile_gatedcrossattention_pb_t_kernel(tc, query, hr, Wu, bu, Wh, bh, out):
         quantise("x", 0)
         passes("h", 1, (0, 1, 2, 3))
         activate("h", 1, (0, 1, 2, 3))
-        turn("h", 2, (0, 1), "back")
-        subtract_query(0, 0)
+        turn("h", 2, (0,), "hT")
+        turn("x", 1, (0, 1), "back")
         passes("x", 0, (0, 1, 2))
+        subtract_query(0, 0)
+        lay("x", 1, 1, scalar_copy)
         lay("h", 2, 0, vector_copy)
-        lay("h", 2, 1, vector_copy)
-        quantise("h", 2)
-        turn("x", 1, (0,), "xT")
+        turn("h", 2, (1,), "hT")
+        turn("h", 3, (0,), "xT")
         activate("x", 0, (0,))
-        lay("x", 1, 0, scalar_copy)
-        turn("h", 3, (0,), "back")
+        lay("h", 2, 1, scalar_copy)
+        lay("x", 1, 0, vector_copy)
+        turn("h", 3, (1,), "hT")
         subtract_query(0, 1)
-        turn("x", 1, (1,), "xT")
-        lay("x", 1, 1, vector_copy)
+        quantise("h", 2, both=True)
 
         for i in range(GROUPS - 2):
             load_rows("h", i + 5)
             load_rows("x", i + 3)
             if i > 0:
-                quantise("h", i + 2)
-                quantise("x", i + 1)
+                quantise("h", i + 2, both=True)
                 activate("x", i, (0,))
             activate("x", i, (1, 2))
             if i == 0:
                 lay("h", 3, 0, scalar_copy)
             turn_back(i - 1, (0, 1))
-            turn("h", i + 3, (1,), "hT")
+            if i > 0:
+                turn("h", i + 3, (1,), "hT")
             lay("h", i + 3, 1, scalar_copy)
             passes("x", i, (3,))
             activate("x", i, (3,))
@@ -269,8 +306,6 @@ def tile_gatedcrossattention_pb_t_kernel(tc, query, hr, Wu, bu, Wh, bh, out):
             passes("h", i + 2, (0, 1))
             activate("h", i + 2, (0, 1))
             subtract_query(i + 1, 0)
-            if i == 0:
-                quantise("x", 1)
             turn("x", i + 2, (0,), "xT")
             turn("h", i + 4, (0,), "hT")
             passes("h", i + 2, (2, 3))
@@ -309,17 +344,19 @@ def tile_gatedcrossattention_pb_t_kernel(tc, query, hr, Wu, bu, Wh, bh, out):
         add_query(last - 2, 2)
         add_query(last - 2, 3)
         store(last - 2)
-        turn_back(last - 1, (0, 1), "xT")
-        turn_back(last - 1, (2, 3))
-        multiply_row_tile(last, 3, nc.vector)
-        for j in range(3):
-            multiply_row_tile(last, j, nc.gpsimd)
-        turn_back(last, (3,), "hT")
+        for j, role in enumerate(("xT", "xT", "hT", "back")):
+            place_query(last - 1, j, role)
+        for j, role in enumerate(("back", "mx", "mx", "mx")):
+            place_query(last, j, role)
         for j in range(TILES):
-            add_query(last - 1, j)
-        store(last - 1)
-        turn_back(last, (0, 1), "xT")
-        turn_back(last, (2,))
-        add_query(last, 3)
-        for j in range(3):
-            add_query(last, j)
+            turn_back_onto_query(last - 1, j)
+        for j in range(TILES):
+            multiply_row_tile(last, j, nc.vector)
+        for j in range(TILES):
+            copy_back(last - 1, j, scalar_copy)
+        for j in range(TILES):
+            turn_back_onto_query(last, j)
+        copy_back(last, 0, vector_copy)
+        copy_back(last, 1, vector_copy)
+        copy_back(last, 2, scalar_copy)
+        copy_back(last, 3, scalar_copy)

@@ -97,12 +97,16 @@ def tile_gatedcrossattention_pb_t_kernel(tc, query, hr, Wu, bu, Wh, bh, out):
                 )
             return tiles[key], width if name == "x" else 0
 
-        def lay(name, g, half, engine):
+        def lay(name, g, half, engine, first_row=0, end_row=HALF):
             if not live(g):
                 return
             tile_, first = operand(grouped, name, g, TILES * GROUP, BF16, "grouped")
             dst = tile_[:].bitcast(F32)[:, first // 2 + half * GROUP:first // 2 + (half + 1) * GROUP]
-            engine(out=dst.rearrange("p (r a) -> p r a", a=2), in_=banks[(name, g, half)][:].rearrange("p (a r) -> p r a", a=2))
+            cut = slice(first_row, end_row)
+            engine(
+                out=dst.rearrange("p (r a) -> p r a", a=2)[:, cut, :],
+                in_=banks[(name, g, half)][:].rearrange("p (a r) -> p r a", a=2)[:, cut, :],
+            )
 
         def quantise(name, g, both=False):
             if live(g):
@@ -317,8 +321,9 @@ def tile_gatedcrossattention_pb_t_kernel(tc, query, hr, Wu, bu, Wh, bh, out):
             add_query(i - 1, 1)
             turn_back(i - 1, (3,))
             lay("x", i + 2, 0, scalar_copy)
+            lay("x", i + 2, 1, vector_copy, 0, 192)
+            lay("x", i + 2, 1, scalar_copy, 192, HALF)
             lay("h", i + 4, 0, scalar_copy)
-            lay("x", i + 2, 1, vector_copy)
             add_query(i - 1, 2)
             add_query(i - 1, 3)
             store(i - 1)

@@ -164,6 +164,11 @@ def tile_gatedcrossattention_pb_t_kernel(tc, query, hr, Wu, bu, Wh, bh, out):
                     d = result[("h", g)][:, half]
                     nc.gpsimd.tensor_tensor(out=d, in0=result[("x", g)][:, half], in1=d, op=ALU.mult)
 
+        def multiply_feature_tiles(g, first, end, engine):
+            cut = slice(first * GROUP, end * GROUP)
+            d = result[("h", g)][:, cut]
+            engine.tensor_tensor(out=d, in0=result[("x", g)][:, cut], in1=d, op=ALU.mult)
+
         def multiply_row_tile(g, j, engine):
             d = result[("h", g)][:].rearrange("p (t r) -> p t r", t=TILES)[:, :, j * P:(j + 1) * P]
             u = result[("x", g)][:].rearrange("p (t r) -> p t r", t=TILES)[:, :, j * P:(j + 1) * P]
@@ -218,6 +223,10 @@ def tile_gatedcrossattention_pb_t_kernel(tc, query, hr, Wu, bu, Wh, bh, out):
             )
             if g == GROUPS - 1:
                 nc.sync.dma_start(out=group_view(out_rows, g)[:, j, :], in_=blended[g][:, cut])
+
+        def store_rows(g, row_tiles):
+            for j in row_tiles:
+                nc.sync.dma_start(out=group_view(out_rows, g)[:, j, :], in_=blended[g][:, j * E:(j + 1) * E])
 
         def store(g):
             if 0 <= g < GROUPS - 1:
@@ -320,9 +329,13 @@ def tile_gatedcrossattention_pb_t_kernel(tc, query, hr, Wu, bu, Wh, bh, out):
             turn_back(i - 1, (2,))
             add_query(i - 1, 1)
             turn_back(i - 1, (3,))
-            lay("x", i + 2, 0, scalar_copy)
-            lay("x", i + 2, 1, vector_copy, 0, 192)
-            lay("x", i + 2, 1, scalar_copy, 192, HALF)
+            if i == 0:
+                lay("x", 2, 0, vector_copy)
+                lay("x", 2, 1, vector_copy)
+            else:
+                lay("x", i + 2, 0, scalar_copy)
+                lay("x", i + 2, 1, vector_copy, 0, 192)
+                lay("x", i + 2, 1, scalar_copy, 192, HALF)
             lay("h", i + 4, 0, scalar_copy)
             add_query(i - 1, 2)
             add_query(i - 1, 3)
@@ -332,36 +345,41 @@ def tile_gatedcrossattention_pb_t_kernel(tc, query, hr, Wu, bu, Wh, bh, out):
         last = GROUPS - 1
         quantise("x", last)
         activate("x", last - 1, (0, 1, 2))
-        turn_back(last - 2, (0, 1))
-        turn_back(last - 2, (2,), "hT")
         passes("x", last - 1, (3,))
+        turn_back(last - 2, (0,))
         activate("x", last - 1, (3,))
-        multiply_gate(last - 1)
+        multiply_feature_tiles(last - 1, 0, 2, nc.gpsimd)
+        multiply_feature_tiles(last - 1, 2, 3, nc.gpsimd)
         passes("x", last, (0, 1, 2))
         activate("x", last, (0, 1, 2))
+        turn_back(last - 2, (1,))
         subtract_query(last, 0)
         add_query(last - 2, 0)
-        turn_back(last - 2, (3,))
         passes("x", last, (3,))
         activate("x", last, (3,))
+        place_query(last - 2, 2, "hT")
+        turn_back_onto_query(last - 2, 2)
+        place_query(last - 2, 3, "back")
+        turn_back_onto_query(last - 2, 3)
         subtract_query(last, 1)
         add_query(last - 2, 1)
-        add_query(last - 2, 2)
-        add_query(last - 2, 3)
-        store(last - 2)
-        for j, role in enumerate(("xT", "xT", "hT", "back")):
+        store_rows(last - 2, (0, 1))
+        multiply_feature_tiles(last - 1, 3, 4, nc.vector)
+        for j in (2, 3):
+            copy_back(last - 2, j, scalar_copy)
+        for j, role in enumerate(("xT", "xT", "mx", "mx")):
             place_query(last - 1, j, role)
-        for j, role in enumerate(("back", "mx", "mx", "mx")):
+        for j, role in enumerate(("mx", "back")):
             place_query(last, j, role)
         for j in range(TILES):
             turn_back_onto_query(last - 1, j)
         for j in range(TILES):
             multiply_row_tile(last, j, nc.vector)
+        for j, role in ((2, "hT"), (3, "back")):
+            place_query(last, j, role)
         for j in range(TILES):
             copy_back(last - 1, j, scalar_copy)
         for j in range(TILES):
             turn_back_onto_query(last, j)
-        copy_back(last, 0, vector_copy)
-        copy_back(last, 1, vector_copy)
-        copy_back(last, 2, scalar_copy)
-        copy_back(last, 3, scalar_copy)
+        for j, engine in enumerate((vector_copy, vector_copy, vector_copy, scalar_copy)):
+            copy_back(last, j, engine)

@@ -22,10 +22,10 @@ FLOPS = 2 * 2 * ROWS * E * E
 
 BANKS = {"xT": 2, "hT": 1, "mx": 3, "back": 2}
 WEIGHTS = {"h": "Wh", "x": "Wu"}
-ROW_SLOTS = {"h": 5, "x": 6}
+ROW_SLOTS = {"h": 6, "x": 6}
 RESULT_SLOTS = {"h": 5, "x": 2}
 OUT_SLOTS = 3
-PAIR_SLOTS = {"grouped": 3, "codes": 2, "scales": 2}
+PAIR_SLOTS = {"grouped": 3, "codes": 3, "scales": 3}
 
 
 def tile_gatedcrossattention_pb_t_kernel(tc, query, hr, Wu, bu, Wh, bh, out):
@@ -88,9 +88,9 @@ def tile_gatedcrossattention_pb_t_kernel(tc, query, hr, Wu, bu, Wh, bh, out):
                 banks[(name, g, half)] = bank
 
         def operand(tiles, name, g, width, dtype, what):
-            key = (name, g) if name in WEIGHTS.values() else g - 2 if name == "h" else g - 1
+            key = (name, g) if name in WEIGHTS.values() else g - 3 if name == "h" else g - 1
             if key not in tiles:
-                label = name if name in WEIGHTS.values() else "pair%d" % (key + 2)
+                label = name if name in WEIGHTS.values() else "pair%d" % (key + 3)
                 tiles[key] = work.tile(
                     [P, width if name in WEIGHTS.values() else 2 * width], dtype, name=what + "_" + label,
                     tag=what + ("_" + name if name in WEIGHTS.values() else ""), bufs=1 if name in WEIGHTS.values() else PAIR_SLOTS[what], align_bytes=64,
@@ -159,10 +159,7 @@ def tile_gatedcrossattention_pb_t_kernel(tc, query, hr, Wu, bu, Wh, bh, out):
 
         def multiply_gate(g):
             if live(g):
-                for t in (0, 2):
-                    half = slice(t * GROUP, (t + 2) * GROUP)
-                    d = result[("h", g)][:, half]
-                    nc.gpsimd.tensor_tensor(out=d, in0=result[("x", g)][:, half], in1=d, op=ALU.mult)
+                nc.gpsimd.tensor_tensor(out=result[("h", g)][:], in0=result[("x", g)][:], in1=result[("h", g)][:], op=ALU.mult)
 
         def multiply_feature_tiles(g, first, end, engine):
             cut = slice(first * GROUP, end * GROUP)
@@ -260,6 +257,7 @@ def tile_gatedcrossattention_pb_t_kernel(tc, query, hr, Wu, bu, Wh, bh, out):
         load_rows("h", 3)
         load_rows("x", 2)
         load_rows("h", 4)
+        load_rows("h", 5)
 
         bias_bank = psum.tile([P, GROUP], F32, name="T_bias", tag="hT", bufs=BANKS["hT"])
         nc.tensor.transpose(bias_bank[:, 0:P], bias_rows[:].bitcast(F32), identity[:])
@@ -296,35 +294,44 @@ def tile_gatedcrossattention_pb_t_kernel(tc, query, hr, Wu, bu, Wh, bh, out):
         activate("x", 0, (0,))
         lay("h", 2, 1, scalar_copy)
         lay("x", 1, 0, vector_copy)
+        passes("x", 0, (3,))
         turn("h", 3, (1,), "hT")
         subtract_query(0, 1)
-        quantise("h", 2, both=True)
+        turn("h", 4, (0,), "xT")
+        quantise("h", 2)
+        lay("h", 3, 0, scalar_copy)
+        lay("h", 3, 1, vector_copy)
+        quantise("h", 3, both=True)
 
         for i in range(GROUPS - 2):
-            load_rows("h", i + 5)
+            load_rows("h", i + 6)
             load_rows("x", i + 3)
             if i > 0:
-                quantise("h", i + 2, both=True)
                 activate("x", i, (0,))
             activate("x", i, (1, 2))
-            if i == 0:
-                lay("h", 3, 0, scalar_copy)
-            turn_back(i - 1, (0, 1))
+            turn("h", i + 4, (1,), "hT")
             if i > 0:
-                turn("h", i + 3, (1,), "hT")
-            lay("h", i + 3, 1, scalar_copy)
-            passes("x", i, (3,))
+                passes("x", i, (3,))
             activate("x", i, (3,))
-            multiply_gate(i)
+            if i == 0:
+                lay("h", 4, 0, scalar_copy)
+            lay("h", i + 4, 1, scalar_copy)
             passes("h", i + 2, (0, 1))
             activate("h", i + 2, (0, 1))
             subtract_query(i + 1, 0)
+            if live(i + 3):
+                if i > 0:
+                    quantise("h", i + 3, both=True)
+            else:
+                quantise("x", i + 1)
+            multiply_gate(i)
+            turn_back(i - 1, (0, 1))
             turn("x", i + 2, (0,), "xT")
-            turn("h", i + 4, (0,), "hT")
             passes("h", i + 2, (2, 3))
             activate("h", i + 2, (2, 3))
             subtract_query(i + 1, 1)
             turn("x", i + 2, (1,), "xT")
+            turn("h", i + 5, (0,), "hT")
             add_query(i - 1, 0)
             turn_back(i - 1, (2,))
             add_query(i - 1, 1)
@@ -336,7 +343,7 @@ def tile_gatedcrossattention_pb_t_kernel(tc, query, hr, Wu, bu, Wh, bh, out):
                 lay("x", i + 2, 0, scalar_copy)
                 lay("x", i + 2, 1, vector_copy, 0, 192)
                 lay("x", i + 2, 1, scalar_copy, 192, HALF)
-            lay("h", i + 4, 0, scalar_copy)
+            lay("h", i + 5, 0, scalar_copy)
             add_query(i - 1, 2)
             add_query(i - 1, 3)
             store(i - 1)
@@ -349,7 +356,6 @@ def tile_gatedcrossattention_pb_t_kernel(tc, query, hr, Wu, bu, Wh, bh, out):
         turn_back(last - 2, (0,))
         activate("x", last - 1, (3,))
         multiply_feature_tiles(last - 1, 0, 2, nc.gpsimd)
-        multiply_feature_tiles(last - 1, 2, 3, nc.gpsimd)
         passes("x", last, (0, 1, 2))
         activate("x", last, (0, 1, 2))
         turn_back(last - 2, (1,))
@@ -364,18 +370,17 @@ def tile_gatedcrossattention_pb_t_kernel(tc, query, hr, Wu, bu, Wh, bh, out):
         subtract_query(last, 1)
         add_query(last - 2, 1)
         store_rows(last - 2, (0, 1))
-        multiply_feature_tiles(last - 1, 3, 4, nc.vector)
+        multiply_feature_tiles(last - 1, 2, 4, nc.vector)
         for j in (2, 3):
             copy_back(last - 2, j, scalar_copy)
         for j, role in enumerate(("xT", "xT", "mx", "mx")):
             place_query(last - 1, j, role)
-        for j, role in enumerate(("mx", "back")):
-            place_query(last, j, role)
+        place_query(last, 0, "mx")
         for j in range(TILES):
             turn_back_onto_query(last - 1, j)
         for j in range(TILES):
             multiply_row_tile(last, j, nc.vector)
-        for j, role in ((2, "hT"), (3, "back")):
+        for j, role in ((1, "back"), (2, "hT"), (3, "back")):
             place_query(last, j, role)
         for j in range(TILES):
             copy_back(last - 1, j, scalar_copy)

@@ -119,7 +119,7 @@ def tile_gatedcrossattention_pb_t_kernel(tc, query, hr, Wu, bu, Wh, bh, out):
                     in_=src[:, first:first + count * TILES * GROUP],
                 )
 
-        def passes(name, g, feature_tiles):
+        def passes(name, g, feature_tiles, role="mx"):
             if not live(g):
                 return
             if feature_tiles[0] == 0:
@@ -127,7 +127,7 @@ def tile_gatedcrossattention_pb_t_kernel(tc, query, hr, Wu, bu, Wh, bh, out):
                     [P, TILES * GROUP], F32, name="result_%s%d" % (name, g), tag="result_" + name, bufs=RESULT_SLOTS[name]
                 )
             for t in feature_tiles:
-                bank = psum.tile([P, GROUP], F32, name="mx_%s%d_%d" % (name, g, t), tag="mx", bufs=BANKS["mx"])
+                bank = psum.tile([P, GROUP], F32, name="mx_%s%d_%d" % (name, g, t), tag=role, bufs=BANKS[role])
                 codes_w, scales_w = codes[(WEIGHTS[name], 0)], scales[(WEIGHTS[name], 0)]
                 words, at = operand(codes, name, g, GROUP, U32, "codes")
                 plane, at = operand(scales, name, g, GROUP, U8, "scales")
@@ -234,8 +234,6 @@ def tile_gatedcrossattention_pb_t_kernel(tc, query, hr, Wu, bu, Wh, bh, out):
         nc.vector.memset(bias_rows[:], 0.0)
         zero = const.tile([P, 1], F32, name="zero")
         nc.vector.memset(zero[:], 0.0)
-        nc.sync.dma_start(out=bias_rows[0:2, :], in_=bu.rearrange("(a c) -> a c", a=2))
-        nc.sync.dma_start(out=bias_rows[2:4, :], in_=bh.rearrange("(a c) -> a c", a=2))
         warm = const.tile([P, 1], F32, name="warm")
         nc.scalar.activation(out=warm[:], in_=zero[:], func=ACT.Sigmoid)
         identity = const.tile([P, P], F32, name="identity")
@@ -249,6 +247,8 @@ def tile_gatedcrossattention_pb_t_kernel(tc, query, hr, Wu, bu, Wh, bh, out):
 
         load_weights("Wh", Wh)
         load_rows("h", 0)
+        nc.sync.dma_start(out=bias_rows[0:2, :], in_=bu.rearrange("(a c) -> a c", a=2))
+        nc.sync.dma_start(out=bias_rows[2:4, :], in_=bh.rearrange("(a c) -> a c", a=2))
         load_weights("Wu", Wu)
         load_rows("h", 1)
         load_rows("x", 0)
@@ -259,22 +259,23 @@ def tile_gatedcrossattention_pb_t_kernel(tc, query, hr, Wu, bu, Wh, bh, out):
         load_rows("h", 4)
         load_rows("h", 5)
 
-        bias_bank = psum.tile([P, GROUP], F32, name="T_bias", tag="hT", bufs=BANKS["hT"])
-        nc.tensor.transpose(bias_bank[:, 0:P], bias_rows[:].bitcast(F32), identity[:])
-        nc.vector.tensor_copy(out=bias[:], in_=bias_bank[:, 0:TILES].bitcast(BF16))
-
         for name, g, role, engines in (
             ("Wh", 0, "xT", (scalar_copy, scalar_copy)),
             ("h", 0, "back", (scalar_copy, scalar_copy)),
             ("Wu", 0, "xT", (scalar_copy, scalar_copy)),
-            ("h", 1, "back", (scalar_copy, vector_copy)),
+            ("h", 1, "back", (vector_copy, scalar_copy)),
         ):
             turn(name, g, (0, 1), role)
+            if name == "Wu":
+                bias_bank = psum.tile([P, GROUP], F32, name="T_bias", tag="hT", bufs=BANKS["hT"])
+                nc.tensor.transpose(bias_bank[:, 0:P], bias_rows[:].bitcast(F32), identity[:])
+                nc.vector.tensor_copy(out=bias[:], in_=bias_bank[:, 0:TILES].bitcast(BF16))
             for half in range(2):
                 lay(name, g, half, engines[half])
             if name != "Wu":
                 quantise(name, g)
-        passes("h", 0, (0, 1, 2, 3))
+        passes("h", 0, (0, 1, 2))
+        passes("h", 0, (3,), "hT")
         activate("h", 0, (0, 1, 2, 3))
         quantise("Wu", 0)
         turn("x", 0, (0, 1), "xT")

@@ -342,8 +342,7 @@ def tile_gatedcrossattention_pb_t_kernel(tc, query, hr, Wu, bu, Wh, bh, out):
                 lay("x", 2, 1, vector_copy)
             else:
                 lay("x", i + 2, 0, scalar_copy)
-                lay("x", i + 2, 1, vector_copy, 0, 192)
-                lay("x", i + 2, 1, scalar_copy, 192, HALF)
+                lay("x", i + 2, 1, vector_copy)
             lay("h", i + 5, 0, scalar_copy)
             add_query(i - 1, 2)
             add_query(i - 1, 3)

@@ -24,6 +24,7 @@ BANKS = {"xT": 2, "hT": 1, "mx": 3, "back": 2}
 WEIGHTS = {"h": "Wh", "x": "Wu"}
 ROW_SLOTS = {"h": 6, "x": 6}
 RESULT_SLOTS = {"h": 5, "x": 2}
+WHOLE_STORES = GROUPS - 4
 OUT_SLOTS = 3
 PAIR_SLOTS = {"grouped": 3, "codes": 3, "scales": 3}
 
@@ -189,8 +190,8 @@ def tile_gatedcrossattention_pb_t_kernel(tc, query, hr, Wu, bu, Wh, bh, out):
             )
             turned[(g, j)] = bank
 
-        def turn_back_onto_query(g, j):
-            for t in range(TILES):
+        def turn_back_onto_query(g, j, first=0, end=TILES):
+            for t in range(first, end):
                 nc.tensor.matmul(
                     turned[(g, j)][:, t * P:(t + 1) * P], lhsT=result[("h", g)][:, t * GROUP + j * P:t * GROUP + (j + 1) * P], rhs=identity[:],
                     is_transpose=True, start=False, stop=t == TILES - 1,
@@ -218,15 +219,11 @@ def tile_gatedcrossattention_pb_t_kernel(tc, query, hr, Wu, bu, Wh, bh, out):
                 in1=loaded[("x", g)][:, cut].rearrange("p (a m e) -> p a m e", a=2, e=2),
                 op=ALU.add,
             )
-            if g == GROUPS - 1:
+            if g >= WHOLE_STORES:
                 nc.sync.dma_start(out=group_view(out_rows, g)[:, j, :], in_=blended[g][:, cut])
 
-        def store_rows(g, row_tiles):
-            for j in row_tiles:
-                nc.sync.dma_start(out=group_view(out_rows, g)[:, j, :], in_=blended[g][:, j * E:(j + 1) * E])
-
         def store(g):
-            if 0 <= g < GROUPS - 1:
+            if 0 <= g < WHOLE_STORES:
                 nc.sync.dma_start(out=group_view(out_rows, g), in_=blended[g][:].rearrange("p (j e) -> p j e", j=TILES))
 
 
@@ -356,35 +353,37 @@ def tile_gatedcrossattention_pb_t_kernel(tc, query, hr, Wu, bu, Wh, bh, out):
         turn_back(last - 2, (0,))
         activate("x", last - 1, (3,))
         multiply_feature_tiles(last - 1, 0, 2, nc.gpsimd)
+        place_query(last - 2, 1, "back")
+        turn_back_onto_query(last - 2, 1)
         passes("x", last, (0, 1, 2))
-        activate("x", last, (0, 1, 2))
-        turn_back(last - 2, (1,))
+        passes("x", last, (3,), "hT")
+        copy_back(last - 2, 1, scalar_copy)
+        activate("x", last, (0, 1, 2, 3))
+        place_query(last - 1, 0, "xT")
         subtract_query(last, 0)
         add_query(last - 2, 0)
-        passes("x", last, (3,))
-        activate("x", last, (3,))
-        place_query(last - 2, 2, "hT")
-        turn_back_onto_query(last - 2, 2)
-        place_query(last - 2, 3, "back")
-        turn_back_onto_query(last - 2, 3)
+        for j in (2, 3):
+            place_query(last - 2, j, "back")
+            turn_back_onto_query(last - 2, j)
         subtract_query(last, 1)
-        add_query(last - 2, 1)
-        store_rows(last - 2, (0, 1))
         multiply_feature_tiles(last - 1, 2, 4, nc.vector)
         for j in (2, 3):
             copy_back(last - 2, j, scalar_copy)
-        for j, role in enumerate(("xT", "xT", "mx", "mx")):
+        for j, role in ((1, "mx"), (2, "mx"), (3, "xT")):
             place_query(last - 1, j, role)
-        place_query(last, 0, "mx")
         for j in range(TILES):
-            turn_back_onto_query(last - 1, j)
+            turn_back_onto_query(last - 1, j, 0, 2)
+        for j in range(TILES):
+            turn_back_onto_query(last - 1, j, 2, 4)
         for j in range(TILES):
             multiply_row_tile(last, j, nc.vector)
-        for j, role in ((1, "back"), (2, "hT"), (3, "back")):
-            place_query(last, j, role)
         for j in range(TILES):
             copy_back(last - 1, j, scalar_copy)
-        for j in range(TILES):
-            turn_back_onto_query(last, j)
-        for j, engine in enumerate((vector_copy, vector_copy, vector_copy, scalar_copy)):
-            copy_back(last, j, engine)
+        turn_back(last, (0,), "mx")
+        turn_back(last, (1,), "hT")
+        turn_back(last, (2,), "back")
+        place_query(last, 3, "back")
+        turn_back_onto_query(last, 3)
+        for j in (0, 1, 2):
+            add_query(last, j)
+        copy_back(last, 3, scalar_copy)

@@ -58,19 +58,25 @@ def tile_gatedcrossattention_pb_t_kernel(tc, query, hr, Wu, bu, Wh, bh, out):
             return flat[g * GROUP:(g + 1) * GROUP, :].rearrange("(p j) e -> p j e", j=TILES)
 
 
-        def load_rows(name, g):
+        def load_rows(name, g, first=0, end=TILES):
             if live(g):
-                tile_ = rows.tile([P, TILES * E], BF16, name="rows_%s%d" % (name, g), tag="rows_" + name, bufs=ROW_SLOTS[name])
-                nc.sync.dma_start(out=tile_[:].rearrange("p (j e) -> p j e", j=TILES), in_=group_view(dram[name], g))
-                loaded[(name, g)] = tile_
+                if (name, g) not in loaded:
+                    loaded[(name, g)] = rows.tile(
+                        [P, TILES * E], BF16, name="rows_%s%d" % (name, g), tag="rows_" + name, bufs=ROW_SLOTS[name]
+                    )
+                nc.sync.dma_start(
+                    out=loaded[(name, g)][:].rearrange("p (j e) -> p j e", j=TILES)[:, first:end, :],
+                    in_=group_view(dram[name], g)[:, first:end, :],
+                )
 
-        def load_weights(name, w):
-            tile_ = const.tile([P, TILES * E], BF16, name="rows_" + name)
-            nc.sync.dma_start(
-                out=tile_[:].rearrange("m (a e k) -> m a e k", a=2, e=2),
-                in_=w.rearrange("(a m e) k -> m a e k", a=2, e=2),
-            )
-            loaded[(name, 0)] = tile_
+        def load_weights(name, w, halves):
+            if (name, 0) not in loaded:
+                loaded[(name, 0)] = const.tile([P, TILES * E], BF16, name="rows_" + name)
+            for a in halves:
+                nc.sync.dma_start(
+                    out=loaded[(name, 0)][:].rearrange("m (a e k) -> m a e k", a=2, e=2)[:, a, :, :],
+                    in_=w.rearrange("(a m e) k -> m a e k", a=2, e=2)[:, a, :, :],
+                )
 
         def turn(name, g, halves, role):
             if not live(g):
@@ -152,10 +158,16 @@ def tile_gatedcrossattention_pb_t_kernel(tc, query, hr, Wu, bu, Wh, bh, out):
                         bias=bias[:, column + t:column + t + 1], scale=1.0,
                     )
 
-        def subtract_query(g, half):
+        def subtract_feature_tile(g, t):
+            tile_, first = operand(grouped, "x", g, TILES * GROUP, BF16, "grouped")
+            c = result[("h", g)][:, t * GROUP:(t + 1) * GROUP]
+            x_t = tile_[:, first:first + TILES * GROUP].rearrange("p (r t) -> p t r", t=TILES)[:, t, :]
+            nc.gpsimd.tensor_tensor(out=c, in0=c, in1=x_t, op=ALU.subtract)
+
+        def subtract_query(g, half, pairs=2):
             if live(g):
-                c = result[("h", g)][:].rearrange("p (a e r) -> p a e r", a=2, e=2)[:, :, :, half * HALF:(half + 1) * HALF]
-                x_t = banks[("x", g, half)][:].bitcast(BF16).rearrange("p (a r e) -> p a e r", a=2, e=2)
+                c = result[("h", g)][:].rearrange("p (a e r) -> p a e r", a=2, e=2)[:, 0:pairs, :, half * HALF:(half + 1) * HALF]
+                x_t = banks[("x", g, half)][:].bitcast(BF16).rearrange("p (a r e) -> p a e r", a=2, e=2)[:, 0:pairs]
                 nc.vector.tensor_tensor(out=c, in0=c, in1=x_t, op=ALU.subtract)
 
         def multiply_gate(g):
@@ -242,11 +254,13 @@ def tile_gatedcrossattention_pb_t_kernel(tc, query, hr, Wu, bu, Wh, bh, out):
         scalar_copy = nc.scalar.copy
         vector_copy = nc.vector.tensor_copy
 
-        load_weights("Wh", Wh)
-        load_rows("h", 0)
+        load_weights("Wh", Wh, (0,))
+        load_rows("h", 0, 0, 2)
+        load_weights("Wh", Wh, (1,))
+        load_rows("h", 0, 2, 4)
         nc.sync.dma_start(out=bias_rows[0:2, :], in_=bu.rearrange("(a c) -> a c", a=2))
         nc.sync.dma_start(out=bias_rows[2:4, :], in_=bh.rearrange("(a c) -> a c", a=2))
-        load_weights("Wu", Wu)
+        load_weights("Wu", Wu, (0, 1))
         load_rows("h", 1)
         load_rows("x", 0)
         load_rows("x", 1)
@@ -256,35 +270,44 @@ def tile_gatedcrossattention_pb_t_kernel(tc, query, hr, Wu, bu, Wh, bh, out):
         load_rows("h", 4)
         load_rows("h", 5)
 
-        for name, g, role, engines in (
-            ("Wh", 0, "xT", (scalar_copy, scalar_copy)),
-            ("h", 0, "back", (scalar_copy, scalar_copy)),
-            ("Wu", 0, "xT", (scalar_copy, scalar_copy)),
-            ("h", 1, "back", (vector_copy, scalar_copy)),
-        ):
-            turn(name, g, (0, 1), role)
-            if name == "Wu":
-                bias_bank = psum.tile([P, GROUP], F32, name="T_bias", tag="hT", bufs=BANKS["hT"])
-                nc.tensor.transpose(bias_bank[:, 0:P], bias_rows[:].bitcast(F32), identity[:])
-                nc.vector.tensor_copy(out=bias[:], in_=bias_bank[:, 0:TILES].bitcast(BF16))
-            for half in range(2):
-                lay(name, g, half, engines[half])
-            if name != "Wu":
-                quantise(name, g)
+        turn("Wh", 0, (0,), "xT")
+        turn("h", 0, (0,), "back")
+        lay("Wh", 0, 0, scalar_copy)
+        turn("Wh", 0, (1,), "xT")
+        turn("h", 0, (1,), "back")
+        lay("h", 0, 0, vector_copy)
+        lay("Wh", 0, 1, scalar_copy)
+        lay("h", 0, 1, scalar_copy)
+        quantise("Wh", 0)
+        quantise("h", 0)
+        turn("Wu", 0, (0, 1), "xT")
+        bias_bank = psum.tile([P, GROUP], F32, name="T_bias", tag="hT", bufs=BANKS["hT"])
+        nc.tensor.transpose(bias_bank[:, 0:P], bias_rows[:].bitcast(F32), identity[:])
+        nc.vector.tensor_copy(out=bias[:], in_=bias_bank[:, 0:TILES].bitcast(BF16))
+        lay("Wu", 0, 0, scalar_copy)
+        lay("Wu", 0, 1, scalar_copy)
+        turn("h", 1, (0, 1), "back")
+        lay("h", 1, 0, vector_copy)
+        lay("h", 1, 1, scalar_copy)
+        quantise("h", 1)
         passes("h", 0, (0, 1, 2))
         passes("h", 0, (3,), "hT")
-        activate("h", 0, (0, 1, 2, 3))
+        activate("h", 0, (0, 1, 2))
         quantise("Wu", 0)
         turn("x", 0, (0, 1), "xT")
         lay("x", 0, 0, vector_copy)
         lay("x", 0, 1, vector_copy)
         quantise("x", 0)
         passes("h", 1, (0, 1, 2, 3))
-        activate("h", 1, (0, 1, 2, 3))
+        activate("h", 1, (0,))
+        activate("h", 0, (3,))
+        activate("h", 1, (1, 2, 3))
+        for t in (3, 2):
+            subtract_feature_tile(0, t)
         turn("h", 2, (0,), "hT")
         turn("x", 1, (0, 1), "back")
         passes("x", 0, (0, 1, 2))
-        subtract_query(0, 0)
+        subtract_query(0, 0, 1)
         lay("x", 1, 1, scalar_copy)
         lay("h", 2, 0, vector_copy)
         turn("h", 2, (1,), "hT")
@@ -294,7 +317,7 @@ def tile_gatedcrossattention_pb_t_kernel(tc, query, hr, Wu, bu, Wh, bh, out):
         lay("x", 1, 0, vector_copy)
         passes("x", 0, (3,))
         turn("h", 3, (1,), "hT")
-        subtract_query(0, 1)
+        subtract_query(0, 1, 1)
         turn("h", 4, (0,), "xT")
         quantise("h", 2)
         lay("h", 3, 0, scalar_copy)
@@ -322,10 +345,12 @@ def tile_gatedcrossattention_pb_t_kernel(tc, query, hr, Wu, bu, Wh, bh, out):
                     quantise("h", i + 3, both=True)
             else:
                 quantise("x", i + 1)
-            multiply_gate(i)
+            multiply_feature_tiles(i, 0, TILES if live(i + 3) else 3, nc.gpsimd)
             turn_back(i - 1, (0, 1))
             turn("x", i + 2, (0,), "xT")
             passes("h", i + 2, (2, 3))
+            if not live(i + 4):
+                passes("x", i + 1, (0,), "hT")
             activate("h", i + 2, (2, 3))
             subtract_query(i + 1, 1)
             turn("x", i + 2, (1,), "xT")
@@ -339,12 +364,14 @@ def tile_gatedcrossattention_pb_t_kernel(tc, query, hr, Wu, bu, Wh, bh, out):
                 lay("x", 2, 1, vector_copy)
             else:
                 lay("x", i + 2, 0, scalar_copy)
-                lay("x", i + 2, 1, vector_copy)
+                lay("x", i + 2, 1, vector_copy if live(i + 5) else scalar_copy)
             lay("h", i + 5, 0, scalar_copy)
             add_query(i - 1, 2)
             add_query(i - 1, 3)
             store(i - 1)
-            passes("x", i + 1, (0, 1, 2))
+            if not live(i + 3):
+                multiply_feature_tiles(i, 3, TILES, nc.vector)
+            passes("x", i + 1, (0, 1, 2) if live(i + 4) else (1, 2))
 
         last = GROUPS - 1
         quantise("x", last)

@@ -330,15 +330,13 @@ def tile_gatedcrossattention_pb_t_kernel(tc, query, hr, Wu, bu, Wh, bh, out):
             if i > 0:
                 activate("x", i, (0,))
             activate("x", i, (1, 2))
-            turn("h", i + 4, (1,), "hT")
             if i > 0:
                 passes("x", i, (3,))
             activate("x", i, (3,))
             if i == 0:
                 lay("h", 4, 0, scalar_copy)
-            lay("h", i + 4, 1, scalar_copy)
-            passes("h", i + 2, (0, 1))
-            activate("h", i + 2, (0, 1))
+            passes("h", i + 2, (0,))
+            activate("h", i + 2, (0,))
             subtract_query(i + 1, 0)
             if live(i + 3):
                 if i > 0:
@@ -346,12 +344,17 @@ def tile_gatedcrossattention_pb_t_kernel(tc, query, hr, Wu, bu, Wh, bh, out):
             else:
                 quantise("x", i + 1)
             multiply_feature_tiles(i, 0, TILES if live(i + 3) else 3, nc.gpsimd)
-            turn_back(i - 1, (0, 1))
+            turn("h", i + 4, (1,), "hT")
+            turn_back(i - 1, (0,))
             turn("x", i + 2, (0,), "xT")
-            passes("h", i + 2, (2, 3))
+            turn_back(i - 1, (1,))
+            lay("h", i + 4, 1, scalar_copy)
+            if i > 0:
+                lay("x", i + 2, 0, scalar_copy)
+            passes("h", i + 2, (1, 2, 3))
             if not live(i + 4):
                 passes("x", i + 1, (0,), "hT")
-            activate("h", i + 2, (2, 3))
+            activate("h", i + 2, (1, 2, 3))
             subtract_query(i + 1, 1)
             turn("x", i + 2, (1,), "xT")
             turn("h", i + 5, (0,), "hT")
@@ -363,7 +366,6 @@ def tile_gatedcrossattention_pb_t_kernel(tc, query, hr, Wu, bu, Wh, bh, out):
                 lay("x", 2, 0, vector_copy)
                 lay("x", 2, 1, vector_copy)
             else:
-                lay("x", i + 2, 0, scalar_copy)
                 lay("x", i + 2, 1, vector_copy if live(i + 5) else scalar_copy)
             lay("h", i + 5, 0, scalar_copy)
             add_query(i - 1, 2)

from contextlib import ExitStack

import concourse.mybir as mybir
from concourse.masks import make_identity

F32 = mybir.dt.float32
BF16 = mybir.dt.bfloat16
U32 = mybir.dt.uint32
U8 = mybir.dt.uint8
FP8X4 = mybir.dt.float8_e4m3fn_x4
ACT = mybir.ActivationFunctionType
ALU = mybir.AluOpType

P = 128
E = 512
ROWS = 2048 * 4
GROUP = 512
GROUPS = ROWS // GROUP
TILES = 4
HALF = GROUP // 2
FLOPS = 2 * 2 * ROWS * E * E

BANKS = {"xT": 2, "hT": 1, "mx": 3, "back": 2}
WEIGHTS = {"h": "Wh", "x": "Wu"}
ROW_SLOTS = {"h": 6, "x": 6}
RESULT_SLOTS = {"h": 5, "x": 2}
WHOLE_STORES = GROUPS - 4
OUT_SLOTS = 3
PAIR_SLOTS = {"grouped": 3, "codes": 3, "scales": 3}


def tile_gatedcrossattention_pb_t_kernel(tc, query, hr, Wu, bu, Wh, bh, out):
    nc = tc.nc
    dram = {"x": query.rearrange("t b e -> (t b) e"), "h": hr.rearrange("t b e -> (t b) e")}
    out_rows = out.rearrange("t b e -> (t b) e")

    with ExitStack() as ctx:
        const = ctx.enter_context(tc.tile_pool(name="const", bufs=1))
        rows = ctx.enter_context(tc.tile_pool(name="rows", bufs=1))
        work = ctx.enter_context(tc.tile_pool(name="work", bufs=1))
        psum = ctx.enter_context(tc.psum_pool(name="psum", bufs=1))
        ctx.enter_context(tc.manual_schedule())

        loaded = {}
        banks = {}
        grouped = {}
        codes = {}
        scales = {}
        sums = {}
        result = {}
        turned = {}
        blended = {}

        def live(g):
            return 0 <= g < GROUPS

        def group_view(flat, g):
            return flat[g * GROUP:(g + 1) * GROUP, :].rearrange("(p j) e -> p j e", j=TILES)


        def load_rows(name, g, first=0, end=TILES):
            if live(g):
                if (name, g) not in loaded:
                    loaded[(name, g)] = rows.tile(
                        [P, TILES * E], BF16, name="rows_%s%d" % (name, g), tag="rows_" + name, bufs=ROW_SLOTS[name]
                    )
                nc.sync.dma_start(
                    out=loaded[(name, g)][:].rearrange("p (j e) -> p j e", j=TILES)[:, first:end, :],
                    in_=group_view(dram[name], g)[:, first:end, :],
                )

        def load_weights(name, w, halves):
            if (name, 0) not in loaded:
                loaded[(name, 0)] = const.tile([P, TILES * E], BF16, name="rows_" + name)
            for a in halves:
                nc.sync.dma_start(
                    out=loaded[(name, 0)][:].rearrange("m (a e k) -> m a e k", a=2, e=2)[:, a, :, :],
                    in_=w.rearrange("(a m e) k -> m a e k", a=2, e=2)[:, a, :, :],
                )

        def turn(name, g, halves, role):
            if not live(g):
                return
            words = loaded[(name, g)][:].bitcast(F32)
            for half in halves:
                bank = psum.tile([P, GROUP], F32, name="T_%s%d_%d" % (name, g, half), tag=role, bufs=BANKS[role])
                for a in range(2):
                    for k in range(2):
                        j = 2 * half + k
                        nc.tensor.transpose(
                            bank[:, a * HALF + k * P:a * HALF + (k + 1) * P],
                            words[:, j * 256 + a * P:j * 256 + (a + 1) * P],
                            identity[:],
                        )
                banks[(name, g, half)] = bank

        def operand(tiles, name, g, width, dtype, what):
            key = (name, g) if name in WEIGHTS.values() else g - 3 if name == "h" else g - 1
            if key not in tiles:
                label = name if name in WEIGHTS.values() else "pair%d" % (key + 3)
                tiles[key] = work.tile(
                    [P, width if name in WEIGHTS.values() else 2 * width], dtype, name=what + "_" + label,
                    tag=what + ("_" + name if name in WEIGHTS.values() else ""), bufs=1 if name in WEIGHTS.values() else PAIR_SLOTS[what], align_bytes=64,
                )
            return tiles[key], width if name == "x" else 0

        def lay(name, g, half, engine, first_row=0, end_row=HALF):
            if not live(g):
                return
            tile_, first = operand(grouped, name, g, TILES * GROUP, BF16, "grouped")
            dst = tile_[:].bitcast(F32)[:, first // 2 + half * GROUP:first // 2 + (half + 1) * GROUP]
            cut = slice(first_row, end_row)
            engine(
                out=dst.rearrange("p (r a) -> p r a", a=2)[:, cut, :],
                in_=banks[(name, g, half)][:].rearrange("p (a r) -> p r a", a=2)[:, cut, :],
            )

        def quantise(name, g, both=False):
            if live(g):
                src, first = operand(grouped, name, g, TILES * GROUP, BF16, "grouped")
                words, at = operand(codes, name, g, GROUP, U32, "codes")
                plane, at = operand(scales, name, g, GROUP, U8, "scales")
                count = 2 if both else 1
                nc.vector.quantize_mx(
                    out=words[:, at:at + count * GROUP].bitcast(FP8X4), scales=plane[:, at:at + count * GROUP],
                    in_=src[:, first:first + count * TILES * GROUP],
                )

        def passes(name, g, feature_tiles, role="mx"):
            if not live(g):
                return
            if feature_tiles[0] == 0:
                result[(name, g)] = work.tile(
                    [P, TILES * GROUP], F32, name="result_%s%d" % (name, g), tag="result_" + name, bufs=RESULT_SLOTS[name]
                )
            for t in feature_tiles:
                bank = psum.tile([P, GROUP], F32, name="mx_%s%d_%d" % (name, g, t), tag=role, bufs=BANKS[role])
                codes_w, scales_w = codes[(WEIGHTS[name], 0)], scales[(WEIGHTS[name], 0)]
                words, at = operand(codes, name, g, GROUP, U32, "codes")
                plane, at = operand(scales, name, g, GROUP, U8, "scales")
                nc.tensor.matmul_mx(
                    out=bank[:],
                    lhsT=codes_w[:, t * P:(t + 1) * P].bitcast(FP8X4),
                    lhsT_scale=scales_w[:, t * P:(t + 1) * P],
                    rhs=words[:, at:at + GROUP].bitcast(FP8X4),
                    rhs_scale=plane[:, at:at + GROUP],
                    start=True,
                    stop=True,
                )
                sums[(name, g, t)] = bank

        def activate(name, g, feature_tiles):
            if live(g):
                func, column = (ACT.Tanh, TILES) if name == "h" else (ACT.Sigmoid, 0)
                for t in feature_tiles:
                    nc.scalar.activation(
                        out=result[(name, g)][:, t * GROUP:(t + 1) * GROUP], in_=sums[(name, g, t)][:], func=func,
                        bias=bias[:, column + t:column + t + 1], scale=1.0,
                    )

        def subtract_feature_tile(g, t):
            tile_, first = operand(grouped, "x", g, TILES * GROUP, BF16, "grouped")
            c = result[("h", g)][:, t * GROUP:(t + 1) * GROUP]
            x_t = tile_[:, first:first + TILES * GROUP].rearrange("p (r t) -> p t r", t=TILES)[:, t, :]
            nc.gpsimd.tensor_tensor(out=c, in0=c, in1=x_t, op=ALU.subtract)

        def subtract_query(g, half, pairs=2):
            if live(g):
                c = result[("h", g)][:].rearrange("p (a e r) -> p a e r", a=2, e=2)[:, 0:pairs, :, half * HALF:(half + 1) * HALF]
                x_t = banks[("x", g, half)][:].bitcast(BF16).rearrange("p (a r e) -> p a e r", a=2, e=2)[:, 0:pairs]
                nc.vector.tensor_tensor(out=c, in0=c, in1=x_t, op=ALU.subtract)

        def multiply_gate(g):
            if live(g):
                nc.gpsimd.tensor_tensor(out=result[("h", g)][:], in0=result[("x", g)][:], in1=result[("h", g)][:], op=ALU.mult)

        def multiply_feature_tiles(g, first, end, engine):
            cut = slice(first * GROUP, end * GROUP)
            d = result[("h", g)][:, cut]
            engine.tensor_tensor(out=d, in0=result[("x", g)][:, cut], in1=d, op=ALU.mult)

        def multiply_row_tile(g, j, engine):
            d = result[("h", g)][:].rearrange("p (t r) -> p t r", t=TILES)[:, :, j * P:(j + 1) * P]
            u = result[("x", g)][:].rearrange("p (t r) -> p t r", t=TILES)[:, :, j * P:(j + 1) * P]
            engine.tensor_tensor(out=d, in0=u, in1=d, op=ALU.mult)

        def turn_back(g, row_tiles, role="back"):
            if live(g):
                for j in row_tiles:
                    bank = psum.tile([P, E], F32, name="back_%d_%d" % (g, j), tag=role, bufs=BANKS[role])
                    for t in range(TILES):
                        nc.tensor.transpose(
                            bank[:, t * P:(t + 1) * P], result[("h", g)][:, t * GROUP + j * P:t * GROUP + (j + 1) * P], identity[:]
                        )
                    turned[(g, j)] = bank

        def place_query(g, j, role):
            bank = psum.tile([P, E], F32, name="back_%d_%d" % (g, j), tag=role, bufs=BANKS[role])
            nc.tensor.matmul(
                bank[:].rearrange("p (a e m) -> p a e m", a=2, e=2), lhsT=identity_bf16[:],
                rhs=loaded[("x", g)][:, j * E:(j + 1) * E].rearrange("p (a m e) -> p a e m", a=2, e=2), start=True, stop=False,
            )
            turned[(g, j)] = bank

        def turn_back_onto_query(g, j, first=0, end=TILES):
            for t in range(first, end):
                nc.tensor.matmul(
                    turned[(g, j)][:, t * P:(t + 1) * P], lhsT=result[("h", g)][:, t * GROUP + j * P:t * GROUP + (j + 1) * P], rhs=identity[:],
                    is_transpose=True, start=False, stop=t == TILES - 1,
                )

        def copy_back(g, j, engine):
            if g not in blended:
                blended[g] = rows.tile([P, TILES * E], F32, name="out_%d" % g, tag="out", bufs=OUT_SLOTS)
            cut = slice(j * E, (j + 1) * E)
            engine(
                out=blended[g][:, cut].rearrange("p (a m e) -> p a m e", a=2, e=2),
                in_=turned[(g, j)][:].rearrange("p (a e m) -> p a m e", a=2, e=2),
            )
            nc.sync.dma_start(out=group_view(out_rows, g)[:, j, :], in_=blended[g][:, cut])

        def add_query(g, j):
            if not live(g):
                return
            if g not in blended:
                blended[g] = rows.tile([P, TILES * E], F32, name="out_%d" % g, tag="out", bufs=OUT_SLOTS)
            cut = slice(j * E, (j + 1) * E)
            nc.vector.tensor_tensor(
                out=blended[g][:, cut].rearrange("p (a m e) -> p a m e", a=2, e=2),
                in0=turned[(g, j)][:].rearrange("p (a e m) -> p a m e", a=2, e=2),
                in1=loaded[("x", g)][:, cut].rearrange("p (a m e) -> p a m e", a=2, e=2),
                op=ALU.add,
            )
            if g >= WHOLE_STORES:
                nc.sync.dma_start(out=group_view(out_rows, g)[:, j, :], in_=blended[g][:, cut])

        def store(g):
            if 0 <= g < WHOLE_STORES:
                nc.sync.dma_start(out=group_view(out_rows, g), in_=blended[g][:].rearrange("p (j e) -> p j e", j=TILES))


        bias_rows = const.tile([P, 2 * P], BF16, name="bias_rows")
        nc.vector.memset(bias_rows[:], 0.0)
        zero = const.tile([P, 1], F32, name="zero")
        nc.vector.memset(zero[:], 0.0)
        warm = const.tile([P, 1], F32, name="warm")
        nc.scalar.activation(out=warm[:], in_=zero[:], func=ACT.Sigmoid)
        identity = const.tile([P, P], F32, name="identity")
        make_identity(nc, identity[:])
        identity_bf16 = const.tile([P, P], BF16, name="identity_bf16")
        nc.gpsimd.tensor_copy(out=identity_bf16[:], in_=identity[:])
        bias = const.tile([P, 2 * TILES], F32, name="bias")

        scalar_copy = nc.scalar.copy
        vector_copy = nc.vector.tensor_copy

        load_weights("Wh", Wh, (0,))
        load_rows("h", 0, 0, 2)
        load_weights("Wh", Wh, (1,))
        load_rows("h", 0, 2, 4)
        nc.sync.dma_start(out=bias_rows[0:2, :], in_=bu.rearrange("(a c) -> a c", a=2))
        nc.sync.dma_start(out=bias_rows[2:4, :], in_=bh.rearrange("(a c) -> a c", a=2))
        load_weights("Wu", Wu, (0, 1))
        load_rows("h", 1)
        load_rows("x", 0)
        load_rows("x", 1)
        load_rows("h", 2)
        load_rows("h", 3)
        load_rows("x", 2)
        load_rows("h", 4)
        load_rows("h", 5)

        turn("Wh", 0, (0,), "xT")
        turn("h", 0, (0,), "back")
        lay("Wh", 0, 0, scalar_copy)
        turn("Wh", 0, (1,), "xT")
        turn("h", 0, (1,), "back")
        lay("h", 0, 0, vector_copy)
        lay("Wh", 0, 1, scalar_copy)
        lay("h", 0, 1, scalar_copy)
        quantise("Wh", 0)
        quantise("h", 0)
        turn("Wu", 0, (0, 1), "xT")
        bias_bank = psum.tile([P, GROUP], F32, name="T_bias", tag="hT", bufs=BANKS["hT"])
        nc.tensor.transpose(bias_bank[:, 0:P], bias_rows[:].bitcast(F32), identity[:])
        nc.vector.tensor_copy(out=bias[:], in_=bias_bank[:, 0:TILES].bitcast(BF16))
        lay("Wu", 0, 0, scalar_copy)
        lay("Wu", 0, 1, scalar_copy)
        turn("h", 1, (0, 1), "back")
        lay("h", 1, 0, vector_copy)
        lay("h", 1, 1, scalar_copy)
        quantise("h", 1)
        passes("h", 0, (0, 1, 2))
        passes("h", 0, (3,), "hT")
        activate("h", 0, (0, 1, 2))
        quantise("Wu", 0)
        turn("x", 0, (0, 1), "xT")
        lay("x", 0, 0, vector_copy)
        lay("x", 0, 1, vector_copy)
        quantise("x", 0)
        passes("h", 1, (0, 1, 2, 3))
        activate("h", 1, (0,))
        activate("h", 0, (3,))
        activate("h", 1, (1, 2, 3))
        for t in (3, 2):
            subtract_feature_tile(0, t)
        turn("h", 2, (0,), "hT")
        turn("x", 1, (0, 1), "back")
        passes("x", 0, (0, 1, 2))
        subtract_query(0, 0, 1)
        lay("x", 1, 1, scalar_copy)
        lay("h", 2, 0, vector_copy)
        turn("h", 2, (1,), "hT")
        turn("h", 3, (0,), "xT")
        activate("x", 0, (0,))
        lay("h", 2, 1, scalar_copy)
        lay("x", 1, 0, vector_copy)
        passes("x", 0, (3,))
        turn("h", 3, (1,), "hT")
        subtract_query(0, 1, 1)
        turn("h", 4, (0,), "xT")
        quantise("h", 2)
        lay("h", 3, 0, scalar_copy)
        lay("h", 3, 1, vector_copy)
        quantise("h", 3, both=True)

        for i in range(GROUPS - 2):
            load_rows("h", i + 6)
            load_rows("x", i + 3)
            if i > 0:
                activate("x", i, (0,))
            activate("x", i, (1, 2))
            if i > 0:
                passes("x", i, (3,))
            activate("x", i, (3,))
            if i == 0:
                lay("h", 4, 0, scalar_copy)
            passes("h", i + 2, (0,))
            activate("h", i + 2, (0,))
            subtract_query(i + 1, 0)
            if live(i + 3):
                if i > 0:
                    quantise("h", i + 3, both=True)
            else:
                quantise("x", i + 1)
            multiply_feature_tiles(i, 0, TILES if live(i + 3) else 3, nc.gpsimd)
            turn("h", i + 4, (1,), "hT")
            turn_back(i - 1, (0,))
            turn("x", i + 2, (0,), "xT")
            turn_back(i - 1, (1,))
            lay("h", i + 4, 1, scalar_copy)
            if i > 0:
                lay("x", i + 2, 0, scalar_copy)
            passes("h", i + 2, (1, 2, 3))
            if not live(i + 4):
                passes("x", i + 1, (0,), "hT")
            activate("h", i + 2, (1, 2, 3))
            subtract_query(i + 1, 1)
            turn("x", i + 2, (1,), "xT")
            turn("h", i + 5, (0,), "hT")
            add_query(i - 1, 0)
            turn_back(i - 1, (2,))
            add_query(i - 1, 1)
            turn_back(i - 1, (3,))
            if i == 0:
                lay("x", 2, 0, vector_copy)
                lay("x", 2, 1, vector_copy)
            else:
                lay("x", i + 2, 1, vector_copy if live(i + 5) else scalar_copy)
            lay("h", i + 5, 0, scalar_copy)
            add_query(i - 1, 2)
            add_query(i - 1, 3)
            store(i - 1)
            if not live(i + 3):
                multiply_feature_tiles(i, 3, TILES, nc.vector)
            passes("x", i + 1, (0, 1, 2) if live(i + 4) else (1, 2))

        last = GROUPS - 1
        quantise("x", last)
        activate("x", last - 1, (0, 1, 2))
        passes("x", last - 1, (3,))
        turn_back(last - 2, (0,))
        activate("x", last - 1, (3,))
        multiply_feature_tiles(last - 1, 0, 2, nc.gpsimd)
        place_query(last - 2, 1, "back")
        turn_back_onto_query(last - 2, 1)
        passes("x", last, (0, 1, 2))
        passes("x", last, (3,), "hT")
        copy_back(last - 2, 1, scalar_copy)
        activate("x", last, (0, 1, 2, 3))
        place_query(last - 1, 0, "xT")
        subtract_query(last, 0)
        add_query(last - 2, 0)
        for j in (2, 3):
            place_query(last - 2, j, "back")
            turn_back_onto_query(last - 2, j)
        subtract_query(last, 1)
        multiply_feature_tiles(last - 1, 2, 4, nc.vector)
        for j in (2, 3):
            copy_back(last - 2, j, scalar_copy)
        for j, role in ((1, "mx"), (2, "mx"), (3, "xT")):
            place_query(last - 1, j, role)
        for j in range(TILES):
            turn_back_onto_query(last - 1, j, 0, 2)
        for j in range(TILES):
            turn_back_onto_query(last - 1, j, 2, 4)
        for j in range(TILES):
            multiply_row_tile(last, j, nc.vector)
        for j in range(TILES):
            copy_back(last - 1, j, scalar_copy)
        turn_back(last, (0,), "mx")
        turn_back(last, (1,), "hT")
        turn_back(last, (2,), "back")
        place_query(last, 3, "back")
        turn_back_onto_query(last, 3)
        for j in (0, 1, 2):
            add_query(last, j)
        copy_back(last, 3, scalar_copy)
